import numpy as np
import ml_dtypes


def mxq(x, axis, fmt="e4m3"):
    dtype, down = {"e4m3": (ml_dtypes.float8_e4m3fn, 7), "e5m2": (ml_dtypes.float8_e5m2, 14)}[fmt]
    v = np.moveaxis(np.asarray(x, np.float32).astype(ml_dtypes.bfloat16).astype(np.float64), axis, -1)
    blocks = v.reshape(v.shape[:-1] + (-1, 32))
    amax = np.abs(blocks).max(-1, keepdims=True)
    byte = np.maximum(np.where(amax > 0, np.frexp(amax)[1] - 1 + 127, 0) - down, 1)
    scale = np.exp2(byte - 127.0)
    codes = (blocks / scale).astype(np.float32).astype(dtype).astype(np.float64)
    return np.moveaxis((codes * scale).reshape(v.shape), -1, axis)


WIDE = False


def mx_kscale(k):
    if not WIDE:
        return np.ones(k)
    levels = np.array([10, -10, 5, -5, 0])
    a = np.random.permutation(np.resize(levels, k // 512 * 4)).reshape(k // 512, 4)
    idx = np.arange(k)
    return np.exp2(a[idx // 512, idx % 128 // 32])


BF16 = ml_dtypes.bfloat16


def bf(x):
    return np.asarray(x, np.float32).astype(BF16)


def f64(x):
    return np.asarray(x).astype(np.float64)


B, L, D, H, DK = 4, 256, 1024, 16, 64
E = H * DK


def tropical_linear(t, w):
    return np.stack([np.max(t[n][:, None, :] + w[None, :, :], axis=-1) for n in range(t.shape[0])])


def split_heads(t):
    return t.reshape(B, L, H, DK).transpose(0, 2, 1, 3).reshape(B * H, L, DK)


def proj(xq, w, lam):
    return np.log1p(np.maximum(xq @ mxq(f64(w), 1, "e4m3").T, 0.0)) - lam


def setup_inputs():
    s = mx_kscale(D)
    return {"x": bf(np.random.standard_normal((B, L, D)) * s),
            "Wq": bf(np.random.standard_normal((E, D)) / np.sqrt(D) / s[None, :]),
            "Wk": bf(np.random.standard_normal((E, D)) / np.sqrt(D) / s[None, :]),
            "Wv": bf(np.random.standard_normal((E, D)) / np.sqrt(D) / s[None, :]),
            "lam": bf(1.0 + 0.1 * np.random.standard_normal((1, 1, E))),
            "Wq_trop": bf(np.random.standard_normal((DK, DK))),
            "Wk_trop": bf(np.random.standard_normal((DK, DK))),
            "Wv_trop": bf(np.random.standard_normal((DK, DK)))}


def reference(x, Wq, Wk, Wv, lam, Wq_trop, Wk_trop, Wv_trop):
    xq = mxq(f64(x), 2, "e4m3")
    lam = f64(lam)
    q = tropical_linear(split_heads(proj(xq, Wq, lam)), f64(Wq_trop))
    k = tropical_linear(split_heads(proj(xq, Wk, lam)), f64(Wk_trop))
    v = tropical_linear(split_heads(proj(xq, Wv, lam)), f64(Wv_trop))
    return q, k, v

@@ -1,0 +1,208 @@
+from contextlib import ExitStack
+
+import concourse.mybir as mybir
+from concourse.masks import make_identity
+
+F32 = mybir.dt.float32
+BF16 = mybir.dt.bfloat16
+U32 = mybir.dt.uint32
+U8 = mybir.dt.uint8
+FP8X4 = mybir.dt.float8_e4m3fn_x4
+ALU = mybir.AluOpType
+ACT = mybir.ActivationFunctionType
+
+P = 128
+ROWS = 1024
+D = 1024
+H = 16
+DK = 64
+CH = 8
+OG = 4
+OHALF = 32
+
+FLOPS = 3 * 2 * ROWS * D * D + 3 * 2 * ROWS * H * DK * DK
+
+
+def tile_tropicalattention_pa_kernel(
+    tc, x, Wq, Wk, Wv, lam, Wq_trop, Wk_trop, Wv_trop, out_0, out_1, out_2
+):
+    nc = tc.nc
+    weights = [Wq, Wk, Wv]
+    outs = [out_0, out_1, out_2]
+    with ExitStack() as ctx:
+        const = ctx.enter_context(tc.tile_pool(name="const", bufs=1))
+        rawp = ctx.enter_context(tc.tile_pool(name="rawp", bufs=2))
+        grp = ctx.enter_context(tc.tile_pool(name="grp", bufs=3))
+        xq = ctx.enter_context(tc.tile_pool(name="xq", bufs=1))
+        wq = ctx.enter_context(tc.tile_pool(name="wq", bufs=2))
+        pp = ctx.enter_context(tc.tile_pool(name="pp", bufs=2))
+        accp = ctx.enter_context(tc.tile_pool(name="accp", bufs=7))
+        yp = ctx.enter_context(tc.tile_pool(name="yp", bufs=2))
+        ps_t = ctx.enter_context(tc.psum_pool(name="ps_t", bufs=2))
+        ps_z = ctx.enter_context(tc.psum_pool(name="ps_z", bufs=2))
+        ps_f = ctx.enter_context(tc.psum_pool(name="ps_f", bufs=4))
+
+        ident = const.tile([P, P], F32, name="ident")
+        make_identity(nc, ident[:])
+
+        x_raw = rawp.tile([P, CH * D], BF16, name="x_raw", tag="raw")
+        x_view = x.rearrange("b (p s) k -> p b (s k)", s=2)
+        x_dst = x_raw[:].rearrange("p (b f) -> p b f", b=4)
+        for half in range(2):
+            nc.sync.dma_start(out=x_dst[:, 2 * half : 2 * half + 2, :], in_=x_view[:, 2 * half : 2 * half + 2, :])
+
+        def load_w(j):
+            w_raw = rawp.tile([P, CH * D], BF16, name="w_raw%d" % j, tag="raw")
+            w_view = weights[j].rearrange("(m c) k -> m (c k)", c=CH)
+            for half in range(2):
+                cols = slice(half * 4 * D, (half + 1) * 4 * D)
+                nc.sync.dma_start(out=w_raw[:, cols], in_=w_view[:, cols])
+            return w_raw
+
+        w_raws = [load_w(0)]
+
+        t_a = const.tile([P, DK], BF16, name="t_a")
+        t_b = const.tile([P, DK], BF16, name="t_b")
+        nc.scalar.dma_start(out=t_a[0:64, :], in_=Wq_trop)
+        nc.scalar.dma_start(out=t_a[64:128, :], in_=Wk_trop)
+        nc.scalar.dma_start(out=t_b[0:64, :], in_=Wv_trop)
+        nc.scalar.dma_start(out=t_b[64:128, :], in_=Wv_trop)
+        lam_sb = const.tile([P, CH], BF16, name="lam_sb")
+        nc.scalar.dma_start(out=lam_sb[:], in_=lam.rearrange("a b (m c) -> (a b m) c", c=CH))
+
+        def quantise(raw, codes, scales, use_vector):
+            rawf = raw[:].bitcast(F32)
+            for g in range(2):
+                grouped = grp.tile([P, 4 * ROWS], BF16, name="grouped", tag="grouped", align_bytes=64)
+                gf = grouped[:].bitcast(F32)
+                for pair in range(4):
+                    tp = ps_t.tile([P, 2, 2, P], F32, name="tp", tag="tp")
+                    for tt in range(2):
+                        for u in range(2):
+                            col = (2 * pair + tt) * 512 + 256 * g + 128 * u
+                            nc.tensor.transpose(tp[:, tt, u, :], rawf[:, col : col + P], ident[:])
+                    dst = gf[:, pair * 512 : (pair + 1) * 512].rearrange("q (t n u) -> q t n u", t=2, u=2)
+                    src = tp[:].rearrange("q t u n -> q t n u")
+                    if use_vector and pair % 2 == 0:
+                        nc.vector.tensor_copy(out=dst, in_=src)
+                    else:
+                        nc.scalar.copy(out=dst, in_=src)
+                for half in range(2):
+                    nc.vector.quantize_mx(
+                        out=codes[g][:, half * 512 : (half + 1) * 512].bitcast(FP8X4),
+                        scales=scales[g][:, half * 512 : (half + 1) * 512],
+                        in_=grouped[:, half * 2048 : (half + 1) * 2048],
+                    )
+
+        x_codes = [xq.tile([P, ROWS], U32, name="x_codes%d" % g, align_bytes=64) for g in range(2)]
+        x_scales = [xq.tile([P, ROWS], U8, name="x_scales%d" % g, align_bytes=64) for g in range(2)]
+        quantise(x_raw, x_codes, x_scales, True)
+
+        lam_f = const.tile([P, CH], F32, name="lam_f")
+        nc.vector.tensor_copy(out=lam_f[:], in_=lam_sb[:])
+        tl = const.tile([P, 3, CH, DK], F32, name="tl")
+        for which, t_sb in enumerate([t_a, t_b]):
+            rep = const.tile([P, CH, H, CH], F32, name="rep%d" % which)
+            nc.vector.tensor_copy(
+                out=rep[:],
+                in_=t_sb[:].rearrange("p (a c) -> p c a", c=CH).unsqueeze(2).to_broadcast([P, CH, H, CH]),
+            )
+            for quad in range(2):
+                tq = ps_t.tile([P, 4, P], F32, name="tq", tag="tp")
+                for cc in range(4):
+                    c = 4 * quad + cc
+                    nc.tensor.transpose(tq[:, cc, :], rep[:, c, :, :].rearrange("p h a -> p (h a)"), ident[:])
+                for cc in range(4):
+                    c = 4 * quad + cc
+                    if which == 0:
+                        nc.vector.tensor_scalar(
+                            out=tl[:, 0:2, c, :],
+                            in0=tq[:, cc, :].rearrange("p (j o) -> p j o", j=2),
+                            scalar1=lam_f[:, c : c + 1],
+                            scalar2=None,
+                            op0=ALU.subtract,
+                        )
+                    else:
+                        nc.vector.tensor_scalar(
+                            out=tl[:, 2, c, :],
+                            in0=tq[:, cc, 0:DK],
+                            scalar1=lam_f[:, c : c + 1],
+                            scalar2=None,
+                            op0=ALU.subtract,
+                        )
+
+        def project(j, w_raw):
+            w_codes = [wq.tile([P, ROWS], U32, name="w_codes%d" % g, align_bytes=64) for g in range(2)]
+            w_scales = [wq.tile([P, ROWS], U8, name="w_scales%d" % g, align_bytes=64) for g in range(2)]
+            quantise(w_raw, w_codes, w_scales, j == 0)
+            pt = pp.tile([P, CH, ROWS], F32, name="pt", tag="pt")
+            for c in range(CH):
+                for rh in range(2):
+                    z = ps_z.tile([P, 512], F32, name="z", tag="z")
+                    for g in range(2):
+                        nc.tensor.matmul_mx(
+                            out=z[:],
+                            lhsT=w_codes[g][:, c * P : (c + 1) * P].bitcast(FP8X4),
+                            lhsT_scale=w_scales[g][:, c * P : (c + 1) * P],
+                            rhs=x_codes[g][:, rh * 512 : (rh + 1) * 512].bitcast(FP8X4),
+                            rhs_scale=x_scales[g][:, rh * 512 : (rh + 1) * 512],
+                            start=(g == 0),
+                            stop=(g == 1),
+                        )
+                    dst = pt[:, c, rh * 512 : (rh + 1) * 512]
+                    if j == 0:
+                        nc.vector.tensor_scalar_max(out=dst, in0=z[:], scalar1=0.0)
+                    else:
+                        nc.scalar.activation(out=dst, in_=z[:], func=ACT.Relu)
+                nc.scalar.activation(out=pt[:, c, :], in_=pt[:, c, :], func=ACT.Ln, bias=1.0, scale=1.0)
+            return pt
+
+        def tropical(j, pt):
+            out_view = outs[j].rearrange("(b h) (p s) o -> p (b h) s o", h=H, s=2)
+            for oh in range(2):
+                y = yp.tile([P, 4, H, 2, OHALF], F32, name="y", tag="y")
+                for og in range(OHALF // OG):
+                    os_ = [oh * OHALF + og * OG + k for k in range(OG)]
+                    accs = []
+                    for o in os_:
+                        acc = accp.tile([P, ROWS], F32, name="acc", tag="acc")
+                        nc.scalar.activation(
+                            out=acc[:], in_=pt[:, 0, :], func=ACT.Identity, bias=tl[:, j, 0, o : o + 1], scale=1.0
+                        )
+                        accs.append(acc)
+                    for c in range(1, CH):
+                        for o, acc in zip(os_, accs):
+                            nc.vector.scalar_tensor_tensor(
+                                out=acc[:],
+                                in0=pt[:, c, :],
+                                scalar=tl[:, j, c, o : o + 1],
+                                in1=acc[:],
+                                op0=ALU.add,
+                                op1=ALU.max,
+                            )
+                    for o, acc in zip(os_, accs):
+                        for bh in range(2):
+                            ft = ps_f.tile([P, 4, P], F32, name="ft", tag="ft")
+                            for tt in range(4):
+                                t = 4 * bh + tt
+                                nc.tensor.transpose(ft[:, tt, :], acc[:, t * P : (t + 1) * P], ident[:])
+                            nc.vector.tensor_reduce(
+                                out=y[:, 2 * bh : 2 * bh + 2, :, :, o - oh * OHALF].rearrange("p b h s -> p b s h"),
+                                in_=ft[:].rearrange("p (b s) (h a) -> p b s h a", s=2, a=CH),
+                                axis=mybir.AxisListType.X,
+                                op=ALU.max,
+                            )
+                y_view = y[:].rearrange("p b h s o -> p (b h) s o")
+                for s in range(2):
+                    nc.sync.dma_start(
+                        out=out_view[:, :, s, oh * OHALF : (oh + 1) * OHALF], in_=y_view[:, :, s, :]
+                    )
+
+        pts = [project(0, w_raws[0])]
+        w_raws.append(load_w(1))
+        pts.append(project(1, w_raws[1]))
+        tropical(0, pts[0])
+        w_raws.append(load_w(2))
+        pts.append(project(2, w_raws[2]))
+        tropical(1, pts[1])
+        tropical(2, pts[2])

@@ -17,8 +17,11 @@ D = 1024
 H = 16
 DK = 64
 CH = 8
-OG = 4
-OHALF = 32
+NPAIR = 4
+VPAIRS = 2
+OQ = 16
+GAP = 128.0
+FLOOR = -3.0e38
 
 FLOPS = 3 * 2 * ROWS * D * D + 3 * 2 * ROWS * H * DK * DK
 
@@ -31,35 +34,37 @@ def tile_tropicalattention_pa_kernel(
     outs = [out_0, out_1, out_2]
     with ExitStack() as ctx:
         const = ctx.enter_context(tc.tile_pool(name="const", bufs=1))
-        rawp = ctx.enter_context(tc.tile_pool(name="rawp", bufs=2))
+        rawp = ctx.enter_context(tc.tile_pool(name="rawp", bufs=3))
         grp = ctx.enter_context(tc.tile_pool(name="grp", bufs=3))
         xq = ctx.enter_context(tc.tile_pool(name="xq", bufs=1))
-        wq = ctx.enter_context(tc.tile_pool(name="wq", bufs=2))
+        wq = ctx.enter_context(tc.tile_pool(name="wq", bufs=1))
         pp = ctx.enter_context(tc.tile_pool(name="pp", bufs=2))
-        accp = ctx.enter_context(tc.tile_pool(name="accp", bufs=7))
+        work = ctx.enter_context(tc.tile_pool(name="work", bufs=3))
         yp = ctx.enter_context(tc.tile_pool(name="yp", bufs=2))
-        ps_t = ctx.enter_context(tc.psum_pool(name="ps_t", bufs=2))
-        ps_z = ctx.enter_context(tc.psum_pool(name="ps_z", bufs=2))
-        ps_f = ctx.enter_context(tc.psum_pool(name="ps_f", bufs=4))
+        psum = ctx.enter_context(tc.psum_pool(name="psum", bufs=8))
 
         ident = const.tile([P, P], F32, name="ident")
         make_identity(nc, ident[:])
 
-        x_raw = rawp.tile([P, CH * D], BF16, name="x_raw", tag="raw")
-        x_view = x.rearrange("b (p s) k -> p b (s k)", s=2)
-        x_dst = x_raw[:].rearrange("p (b f) -> p b f", b=4)
-        for half in range(2):
-            nc.sync.dma_start(out=x_dst[:, 2 * half : 2 * half + 2, :], in_=x_view[:, 2 * half : 2 * half + 2, :])
+        def load_halves(view, label):
+            halves = []
+            for half in range(2):
+                raw = rawp.tile([P, 4 * D], BF16, name="%s%d" % (label, half), tag="raw")
+                nc.sync.dma_start(out=raw[:], in_=view[:, half * 4 * D : (half + 1) * 4 * D])
+                halves.append(raw)
+            return halves
 
         def load_w(j):
-            w_raw = rawp.tile([P, CH * D], BF16, name="w_raw%d" % j, tag="raw")
-            w_view = weights[j].rearrange("(m c) k -> m (c k)", c=CH)
-            for half in range(2):
-                cols = slice(half * 4 * D, (half + 1) * 4 * D)
-                nc.sync.dma_start(out=w_raw[:, cols], in_=w_view[:, cols])
-            return w_raw
+            return load_halves(weights[j].rearrange("(m c) k -> m (c k)", c=CH), "w_raw")
 
-        w_raws = [load_w(0)]
+        x_raw = []
+        x_view = x.rearrange("b (p s) k -> p b (s k)", s=2)
+        for half in range(2):
+            raw = rawp.tile([P, 4 * D], BF16, name="x_raw%d" % half, tag="raw")
+            nc.sync.dma_start(
+                out=raw[:].rearrange("p (b f) -> p b f", b=2), in_=x_view[:, 2 * half : 2 * half + 2, :]
+            )
+            x_raw.append(raw)
 
         t_a = const.tile([P, DK], BF16, name="t_a")
         t_b = const.tile([P, DK], BF16, name="t_b")
@@ -70,45 +75,46 @@ def tile_tropicalattention_pa_kernel(
         lam_sb = const.tile([P, CH], BF16, name="lam_sb")
         nc.scalar.dma_start(out=lam_sb[:], in_=lam.rearrange("a b (m c) -> (a b m) c", c=CH))
 
-        def quantise(raw, codes, scales, use_vector):
-            rawf = raw[:].bitcast(F32)
-            for g in range(2):
-                grouped = grp.tile([P, 4 * ROWS], BF16, name="grouped", tag="grouped", align_bytes=64)
-                gf = grouped[:].bitcast(F32)
-                for pair in range(4):
-                    tp = ps_t.tile([P, 2, 2, P], F32, name="tp", tag="tp")
-                    for tt in range(2):
-                        for u in range(2):
-                            col = (2 * pair + tt) * 512 + 256 * g + 128 * u
-                            nc.tensor.transpose(tp[:, tt, u, :], rawf[:, col : col + P], ident[:])
-                    dst = gf[:, pair * 512 : (pair + 1) * 512].rearrange("q (t n u) -> q t n u", t=2, u=2)
-                    src = tp[:].rearrange("q t u n -> q t n u")
-                    if use_vector and pair % 2 == 0:
-                        nc.vector.tensor_copy(out=dst, in_=src)
-                    else:
-                        nc.scalar.copy(out=dst, in_=src)
-                for half in range(2):
+        def quantise(raws, codes, scales, use_vector):
+            for half in range(2):
+                rawf = raws[half][:].bitcast(F32)
+                for g in range(2):
+                    grouped = grp.tile([P, 2048], BF16, name="grouped", tag="grouped", align_bytes=64)
+                    gf = grouped[:].bitcast(F32)
+                    for pair in range(2):
+                        tp = psum.tile([P, 2, 2, P], F32, name="tp", tag="bank")
+                        for tt in range(2):
+                            for u in range(2):
+                                col = (2 * pair + tt) * 512 + 256 * g + 128 * u
+                                nc.tensor.transpose(tp[:, tt, u, :], rawf[:, col : col + P], ident[:])
+                        dst = gf[:, pair * 512 : (pair + 1) * 512].rearrange("q (t n u) -> q t n u", t=2, u=2)
+                        src = tp[:].rearrange("q t u n -> q t n u")
+                        if use_vector and pair == 0:
+                            nc.vector.tensor_copy(out=dst, in_=src)
+                        else:
+                            nc.scalar.copy(out=dst, in_=src)
                     nc.vector.quantize_mx(
                         out=codes[g][:, half * 512 : (half + 1) * 512].bitcast(FP8X4),
                         scales=scales[g][:, half * 512 : (half + 1) * 512],
-                        in_=grouped[:, half * 2048 : (half + 1) * 2048],
+                        in_=grouped[:],
                     )
 
         x_codes = [xq.tile([P, ROWS], U32, name="x_codes%d" % g, align_bytes=64) for g in range(2)]
         x_scales = [xq.tile([P, ROWS], U8, name="x_scales%d" % g, align_bytes=64) for g in range(2)]
         quantise(x_raw, x_codes, x_scales, True)
+        w_raws = [load_w(0)]
 
         lam_f = const.tile([P, CH], F32, name="lam_f")
         nc.vector.tensor_copy(out=lam_f[:], in_=lam_sb[:])
         tl = const.tile([P, 3, CH, DK], F32, name="tl")
         for which, t_sb in enumerate([t_a, t_b]):
-            rep = const.tile([P, CH, H, CH], F32, name="rep%d" % which)
+            rep = const.tile([P, CH, H, CH], F32, name="rep", tag="rep")
             nc.vector.tensor_copy(
                 out=rep[:],
                 in_=t_sb[:].rearrange("p (a c) -> p c a", c=CH).unsqueeze(2).to_broadcast([P, CH, H, CH]),
             )
             for quad in range(2):
-                tq = ps_t.tile([P, 4, P], F32, name="tq", tag="tp")
+                tq = psum.tile([P, 4, P], F32, name="tq", tag="bank")
                 for cc in range(4):
                     c = 4 * quad + cc
                     nc.tensor.transpose(tq[:, cc, :], rep[:, c, :, :].rearrange("p h a -> p (h a)"), ident[:])
@@ -130,6 +136,23 @@ def tile_tropicalattention_pa_kernel(
                             scalar2=None,
                             op0=ALU.subtract,
                         )
+        SP = NPAIR - VPAIRS
+        fl = const.tile([P, 3, SP, 2, DK], F32, name="fl")
+        nc.vector.tensor_scalar_max(
+            out=fl[:].rearrange("p j q e o -> p j (q e o)"),
+            in0=tl[:, :, 2 * VPAIRS : CH, :].rearrange("p j c o -> p j (c o)"),
+            scalar1=FLOOR,
+        )
+        ta = const.tile([P, 3, SP, DK], F32, name="ta")
+        tb = const.tile([P, 3, SP, DK], F32, name="tb")
+        dt = const.tile([P, 3, SP, DK], F32, name="dt")
+        nc.vector.scalar_tensor_tensor(
+            out=ta[:], in0=fl[:, :, :, 1, :], scalar=-GAP, in1=fl[:, :, :, 0, :], op0=ALU.add, op1=ALU.max
+        )
+        nc.vector.scalar_tensor_tensor(
+            out=tb[:], in0=fl[:, :, :, 0, :], scalar=-GAP, in1=fl[:, :, :, 1, :], op0=ALU.add, op1=ALU.max
+        )
+        nc.vector.tensor_tensor(out=dt[:], in0=tb[:], in1=ta[:], op=ALU.subtract)
 
         def project(j, w_raw):
             w_codes = [wq.tile([P, ROWS], U32, name="w_codes%d" % g, align_bytes=64) for g in range(2)]
@@ -138,7 +161,7 @@ def tile_tropicalattention_pa_kernel(
             pt = pp.tile([P, CH, ROWS], F32, name="pt", tag="pt")
             for c in range(CH):
                 for rh in range(2):
-                    z = ps_z.tile([P, 512], F32, name="z", tag="z")
+                    z = psum.tile([P, 512], F32, name="z", tag="bank")
                     for g in range(2):
                         nc.tensor.matmul_mx(
                             out=z[:],
@@ -155,48 +178,66 @@ def tile_tropicalattention_pa_kernel(
                     else:
                         nc.scalar.activation(out=dst, in_=z[:], func=ACT.Relu)
                 nc.scalar.activation(out=pt[:, c, :], in_=pt[:, c, :], func=ACT.Ln, bias=1.0, scale=1.0)
+                if c % 2 == 1:
+                    eng = nc.vector if j == 0 else nc.gpsimd
+                    eng.tensor_tensor(out=pt[:, c, :], in0=pt[:, c, :], in1=pt[:, c - 1, :], op=ALU.subtract)
             return pt
 
         def tropical(j, pt):
-            out_view = outs[j].rearrange("(b h) (p s) o -> p (b h) s o", h=H, s=2)
-            for oh in range(2):
-                y = yp.tile([P, 4, H, 2, OHALF], F32, name="y", tag="y")
-                for og in range(OHALF // OG):
-                    os_ = [oh * OHALF + og * OG + k for k in range(OG)]
-                    accs = []
-                    for o in os_:
-                        acc = accp.tile([P, ROWS], F32, name="acc", tag="acc")
-                        nc.scalar.activation(
-                            out=acc[:], in_=pt[:, 0, :], func=ACT.Identity, bias=tl[:, j, 0, o : o + 1], scale=1.0
-                        )
-                        accs.append(acc)
-                    for c in range(1, CH):
-                        for o, acc in zip(os_, accs):
-                            nc.vector.scalar_tensor_tensor(
-                                out=acc[:],
-                                in0=pt[:, c, :],
-                                scalar=tl[:, j, c, o : o + 1],
-                                in1=acc[:],
+            out_view = outs[j].rearrange("n (p s) o -> p n s o", s=2)
+            for oq in range(DK // OQ):
+                y = yp.tile([P, 4, H, 2, OQ], F32, name="y", tag="y")
+                for ol in range(OQ):
+                    o = oq * OQ + ol
+                    first = []
+                    second = []
+                    for q in range(NPAIR):
+                        if q < VPAIRS:
+                            gv = work.tile([P, ROWS], F32, name="gv", tag="gv%d" % q)
+                            nc.vector.tensor_scalar(
+                                out=gv[:],
+                                in0=pt[:, 2 * q + 1, :],
+                                scalar1=tl[:, j, 2 * q + 1, o : o + 1],
+                                scalar2=tl[:, j, 2 * q, o : o + 1],
                                 op0=ALU.add,
                                 op1=ALU.max,
                             )
-                    for o, acc in zip(os_, accs):
-                        for bh in range(2):
-                            ft = ps_f.tile([P, 4, P], F32, name="ft", tag="ft")
-                            for tt in range(4):
-                                t = 4 * bh + tt
-                                nc.tensor.transpose(ft[:, tt, :], acc[:, t * P : (t + 1) * P], ident[:])
-                            nc.vector.tensor_reduce(
-                                out=y[:, 2 * bh : 2 * bh + 2, :, :, o - oh * OHALF].rearrange("p b h s -> p b s h"),
-                                in_=ft[:].rearrange("p (b s) (h a) -> p b s h a", s=2, a=CH),
-                                axis=mybir.AxisListType.X,
-                                op=ALU.max,
+                            first.append(pt[:, 2 * q, :])
+                            second.append(gv[:])
+                        else:
+                            us = work.tile([P, ROWS], F32, name="us", tag="us%d" % q)
+                            gs = work.tile([P, ROWS], F32, name="gs", tag="gs%d" % q)
+                            nc.scalar.activation(
+                                out=us[:], in_=pt[:, 2 * q, :], func=ACT.Identity,
+                                bias=ta[:, j, q - VPAIRS, o : o + 1], scale=1.0,
                             )
+                            nc.scalar.activation(
+                                out=gs[:], in_=pt[:, 2 * q + 1, :], func=ACT.Relu,
+                                bias=dt[:, j, q - VPAIRS, o : o + 1], scale=1.0,
+                            )
+                            first.append(us[:])
+                            second.append(gs[:])
+                    for t in range(8):
+                        ft = psum.tile([P, NPAIR, P], F32, name="ft", tag="bank")
+                        cols = slice(t * P, (t + 1) * P)
+                        for q in range(NPAIR):
+                            nc.tensor.matmul(
+                                out=ft[:, q, :], lhsT=first[q][:, cols], rhs=ident[:],
+                                start=True, stop=False, is_transpose=True,
+                            )
+                            nc.tensor.matmul(
+                                out=ft[:, q, :], lhsT=second[q][:, cols], rhs=ident[:],
+                                start=False, stop=True, is_transpose=True,
+                            )
+                        nc.vector.tensor_reduce(
+                            out=y[:, t // 2, :, t % 2, ol],
+                            in_=ft[:].rearrange("p q (h a) -> p h q a", a=CH),
+                            axis=mybir.AxisListType.XY,
+                            op=ALU.max,
+                        )
                 y_view = y[:].rearrange("p b h s o -> p (b h) s o")
                 for s in range(2):
-                    nc.sync.dma_start(
-                        out=out_view[:, :, s, oh * OHALF : (oh + 1) * OHALF], in_=y_view[:, :, s, :]
-                    )
+                    nc.sync.dma_start(out=out_view[:, :, s, oq * OQ : (oq + 1) * OQ], in_=y_view[:, :, s, :])
 
         pts = [project(0, w_raws[0])]
         w_raws.append(load_w(1))

@@ -18,7 +18,7 @@ H = 16
 DK = 64
 CH = 8
 NPAIR = 4
-VPAIRS = 2
+VPAIRS = 1
 OQ = 16
 GAP = 128.0
 FLOOR = -3.0e38
@@ -34,8 +34,8 @@ def tile_tropicalattention_pa_kernel(
     outs = [out_0, out_1, out_2]
     with ExitStack() as ctx:
         const = ctx.enter_context(tc.tile_pool(name="const", bufs=1))
-        rawp = ctx.enter_context(tc.tile_pool(name="rawp", bufs=3))
-        grp = ctx.enter_context(tc.tile_pool(name="grp", bufs=3))
+        rawp = ctx.enter_context(tc.tile_pool(name="rawp", bufs=2))
+        grp = ctx.enter_context(tc.tile_pool(name="grp", bufs=2))
         xq = ctx.enter_context(tc.tile_pool(name="xq", bufs=1))
         wq = ctx.enter_context(tc.tile_pool(name="wq", bufs=1))
         pp = ctx.enter_context(tc.tile_pool(name="pp", bufs=2))
@@ -207,10 +207,17 @@ def tile_tropicalattention_pa_kernel(
                         else:
                             us = work.tile([P, ROWS], F32, name="us", tag="us%d" % q)
                             gs = work.tile([P, ROWS], F32, name="gs", tag="gs%d" % q)
-                            nc.scalar.activation(
-                                out=us[:], in_=pt[:, 2 * q, :], func=ACT.Identity,
-                                bias=ta[:, j, q - VPAIRS, o : o + 1], scale=1.0,
-                            )
+                            if q == VPAIRS:
+                                nc.scalar.activation(
+                                    out=us[:], in_=pt[:, 2 * q, :], func=ACT.Identity,
+                                    bias=ta[:, j, q - VPAIRS, o : o + 1], scale=1.0,
+                                )
+                            else:
+                                nc.gpsimd.tensor_scalar(
+                                    out=us[:], in0=pt[:, 2 * q, :],
+                                    scalar1=ta[:, j, q - VPAIRS, o : o + 1], scalar2=1.0,
+                                    op0=ALU.add, op1=ALU.mult,
+                                )
                             nc.scalar.activation(
                                 out=gs[:], in_=pt[:, 2 * q + 1, :], func=ACT.Relu,
                                 bias=dt[:, j, q - VPAIRS, o : o + 1], scale=1.0,

@@ -18,7 +18,6 @@ H = 16
 DK = 64
 CH = 8
 NPAIR = 4
-VPAIRS = 1
 OQ = 16
 GAP = 128.0
 FLOOR = -3.0e38
@@ -39,9 +38,11 @@ def tile_tropicalattention_pa_kernel(
         xq = ctx.enter_context(tc.tile_pool(name="xq", bufs=1))
         wq = ctx.enter_context(tc.tile_pool(name="wq", bufs=1))
         pp = ctx.enter_context(tc.tile_pool(name="pp", bufs=2))
-        work = ctx.enter_context(tc.tile_pool(name="work", bufs=3))
+        work = ctx.enter_context(tc.tile_pool(name="work", bufs=18))
+        rowp = ctx.enter_context(tc.tile_pool(name="rowp", bufs=1))
         yp = ctx.enter_context(tc.tile_pool(name="yp", bufs=2))
-        psum = ctx.enter_context(tc.psum_pool(name="psum", bufs=8))
+        psum = ctx.enter_context(tc.psum_pool(name="psum", bufs=4))
+        resid = ctx.enter_context(tc.psum_pool(name="resid", bufs=1))
 
         ident = const.tile([P, P], F32, name="ident")
         make_identity(nc, ident[:])
@@ -75,34 +76,33 @@ def tile_tropicalattention_pa_kernel(
         lam_sb = const.tile([P, CH], BF16, name="lam_sb")
         nc.scalar.dma_start(out=lam_sb[:], in_=lam.rearrange("a b (m c) -> (a b m) c", c=CH))
 
-        def quantise(raws, codes, scales, use_vector):
-            for half in range(2):
-                rawf = raws[half][:].bitcast(F32)
-                for g in range(2):
-                    grouped = grp.tile([P, 2048], BF16, name="grouped", tag="grouped", align_bytes=64)
-                    gf = grouped[:].bitcast(F32)
-                    for pair in range(2):
-                        tp = psum.tile([P, 2, 2, P], F32, name="tp", tag="bank")
-                        for tt in range(2):
-                            for u in range(2):
-                                col = (2 * pair + tt) * 512 + 256 * g + 128 * u
-                                nc.tensor.transpose(tp[:, tt, u, :], rawf[:, col : col + P], ident[:])
-                        dst = gf[:, pair * 512 : (pair + 1) * 512].rearrange("q (t n u) -> q t n u", t=2, u=2)
-                        src = tp[:].rearrange("q t u n -> q t n u")
-                        if use_vector and pair == 0:
-                            nc.vector.tensor_copy(out=dst, in_=src)
-                        else:
-                            nc.scalar.copy(out=dst, in_=src)
-                    nc.vector.quantize_mx(
-                        out=codes[g][:, half * 512 : (half + 1) * 512].bitcast(FP8X4),
-                        scales=scales[g][:, half * 512 : (half + 1) * 512],
-                        in_=grouped[:],
-                    )
+        def quantise_part(raws, codes, scales, use_vector, half, g):
+            rawf = raws[half][:].bitcast(F32)
+            grouped = grp.tile([P, 2048], BF16, name="grouped", tag="grouped", align_bytes=64)
+            gf = grouped[:].bitcast(F32)
+            for pair in range(2):
+                tp = psum.tile([P, 2, 2, P], F32, name="tp", tag="bank")
+                for tt in range(2):
+                    for u in range(2):
+                        col = (2 * pair + tt) * 512 + 256 * g + 128 * u
+                        nc.tensor.transpose(tp[:, tt, u, :], rawf[:, col : col + P], ident[:])
+                dst = gf[:, pair * 512 : (pair + 1) * 512].rearrange("q (t n u) -> q t n u", t=2, u=2)
+                src = tp[:].rearrange("q t u n -> q t n u")
+                if use_vector and pair == 0:
+                    nc.vector.tensor_copy(out=dst, in_=src)
+                else:
+                    nc.scalar.copy(out=dst, in_=src)
+            nc.vector.quantize_mx(
+                out=codes[g][:, half * 512 : (half + 1) * 512].bitcast(FP8X4),
+                scales=scales[g][:, half * 512 : (half + 1) * 512],
+                in_=grouped[:],
+            )
 
         x_codes = [xq.tile([P, ROWS], U32, name="x_codes%d" % g, align_bytes=64) for g in range(2)]
         x_scales = [xq.tile([P, ROWS], U8, name="x_scales%d" % g, align_bytes=64) for g in range(2)]
-        quantise(x_raw, x_codes, x_scales, True)
-        w_raws = [load_w(0)]
+        for half in range(2):
+            for g in range(2):
+                quantise_part(x_raw, x_codes, x_scales, True, half, g)
 
         lam_f = const.tile([P, CH], F32, name="lam_f")
         nc.vector.tensor_copy(out=lam_f[:], in_=lam_sb[:])
@@ -136,30 +136,50 @@ def tile_tropicalattention_pa_kernel(
                             scalar2=None,
                             op0=ALU.subtract,
                         )
-        SP = NPAIR - VPAIRS
-        fl = const.tile([P, 3, SP, 2, DK], F32, name="fl")
+        fl = const.tile([P, 3, CH, DK], F32, name="fl")
         nc.vector.tensor_scalar_max(
-            out=fl[:].rearrange("p j q e o -> p j (q e o)"),
-            in0=tl[:, :, 2 * VPAIRS : CH, :].rearrange("p j c o -> p j (c o)"),
-            scalar1=FLOOR,
+            out=fl[:].rearrange("p j c o -> p (j c o)"), in0=tl[:].rearrange("p j c o -> p (j c o)"), scalar1=FLOOR
         )
-        ta = const.tile([P, 3, SP, DK], F32, name="ta")
-        tb = const.tile([P, 3, SP, DK], F32, name="tb")
-        dt = const.tile([P, 3, SP, DK], F32, name="dt")
+        ta = const.tile([P, 3, NPAIR, DK], F32, name="ta")
+        dt = const.tile([P, 3, NPAIR, DK], F32, name="dt")
+        for j in range(3):
+            even = fl[:, j, :, :].rearrange("p (q e) o -> p q e o", e=2)[:, :, 0, :]
+            odd = fl[:, j, :, :].rearrange("p (q e) o -> p q e o", e=2)[:, :, 1, :]
+            nc.vector.scalar_tensor_tensor(
+                out=ta[:, j, :, :], in0=odd, scalar=-GAP, in1=even, op0=ALU.add, op1=ALU.max
+            )
+            nc.vector.scalar_tensor_tensor(
+                out=dt[:, j, :, :], in0=even, scalar=-GAP, in1=odd, op0=ALU.add, op1=ALU.max
+            )
+        nc.vector.tensor_tensor(out=dt[:], in0=dt[:], in1=ta[:], op=ALU.subtract)
+        top = const.tile([P, 3, DK], F32, name="top")
+        nc.vector.tensor_tensor(out=top[:], in0=fl[:, :, 0, :], in1=fl[:, :, 1, :], op=ALU.max)
+        for c in (2, 3):
+            nc.vector.tensor_tensor(out=top[:], in0=top[:], in1=fl[:, :, c, :], op=ALU.max)
+        qa = const.tile([P, 3, DK], F32, name="qa")
+        qd = const.tile([P, 3, 3, DK], F32, name="qd")
         nc.vector.scalar_tensor_tensor(
-            out=ta[:], in0=fl[:, :, :, 1, :], scalar=-GAP, in1=fl[:, :, :, 0, :], op0=ALU.add, op1=ALU.max
+            out=qa[:], in0=top[:], scalar=-GAP, in1=fl[:, :, 0, :], op0=ALU.add, op1=ALU.max
         )
-        nc.vector.scalar_tensor_tensor(
-            out=tb[:], in0=fl[:, :, :, 0, :], scalar=-GAP, in1=fl[:, :, :, 1, :], op0=ALU.add, op1=ALU.max
-        )
-        nc.vector.tensor_tensor(out=dt[:], in0=tb[:], in1=ta[:], op=ALU.subtract)
+        for c in (1, 2, 3):
+            nc.vector.scalar_tensor_tensor(
+                out=qd[:, c - 1, :, :], in0=top[:], scalar=-GAP, in1=fl[:, :, c, :], op0=ALU.add, op1=ALU.max
+            )
+            nc.vector.tensor_tensor(
+                out=qd[:, c - 1, :, :], in0=qd[:, c - 1, :, :], in1=qa[:], op=ALU.subtract
+            )
 
-        def project(j, w_raw):
+        def projection(j):
             w_codes = [wq.tile([P, ROWS], U32, name="w_codes%d" % g, align_bytes=64) for g in range(2)]
             w_scales = [wq.tile([P, ROWS], U8, name="w_scales%d" % g, align_bytes=64) for g in range(2)]
-            quantise(w_raw, w_codes, w_scales, j == 0)
             pt = pp.tile([P, CH, ROWS], F32, name="pt", tag="pt")
-            for c in range(CH):
+            raws = load_w(j)
+            steps = []
+
+            def diff_engine():
+                return nc.vector if j == 0 else nc.gpsimd
+
+            def chunk(c):
                 for rh in range(2):
                     z = psum.tile([P, 512], F32, name="z", tag="bank")
                     for g in range(2):
@@ -178,79 +198,126 @@ def tile_tropicalattention_pa_kernel(
                     else:
                         nc.scalar.activation(out=dst, in_=z[:], func=ACT.Relu)
                 nc.scalar.activation(out=pt[:, c, :], in_=pt[:, c, :], func=ACT.Ln, bias=1.0, scale=1.0)
+                if c in (2, 3):
+                    tmp = work.tile([P, ROWS], F32, name="tmp", tag="u")
+                    diff_engine().tensor_tensor(out=tmp[:], in0=pt[:, c, :], in1=pt[:, 0, :], op=ALU.subtract)
+                    turn(c - 2, tmp)
                 if c % 2 == 1:
-                    eng = nc.vector if j == 0 else nc.gpsimd
-                    eng.tensor_tensor(out=pt[:, c, :], in0=pt[:, c, :], in1=pt[:, c - 1, :], op=ALU.subtract)
-            return pt
+                    diff_engine().tensor_tensor(out=pt[:, c, :], in0=pt[:, c, :], in1=pt[:, c - 1, :], op=ALU.subtract)
 
-        def tropical(j, pt):
+            def turn(k, tmp):
+                rows = rowp.tile([P, ROWS], F32, name="rows", tag="rows%d" % k)
+                for half in range(2):
+                    bank = psum.tile([P, 4, P], F32, name="tr", tag="bank")
+                    for t in range(4):
+                        col = (4 * half + t) * P
+                        nc.tensor.transpose(bank[:, t, :], tmp[:, col : col + P], ident[:])
+                    nc.scalar.copy(out=rows[:, half * 512 : (half + 1) * 512], in_=bank[:].rearrange("p t n -> p (t n)"))
+                turned.append(rows)
+
+            turned = []
+            for half in range(2):
+                for g in range(2):
+                    steps.append(
+                        lambda half=half, g=g: quantise_part(raws, w_codes, w_scales, j == 0, half, g)
+                    )
+            for c in range(CH):
+                steps.append(lambda c=c: chunk(c))
+            return pt, steps, turned
+
+        def settle(turned):
+            banks = []
+            for k in range(2):
+                for half in range(2):
+                    bank = resid.tile([P, 4, P], F32, name="far%d%d" % (k, half), tag="far%d%d" % (k, half))
+                    for t in range(4):
+                        col = (4 * half + t) * P
+                        nc.tensor.transpose(bank[:, t, :], turned[k][:, col : col + P], ident[:])
+                    banks.append(bank)
+            return banks
+
+        def affine(eng, out, in_, col):
+            if eng == "S":
+                nc.scalar.activation(out=out, in_=in_, func=ACT.Identity, bias=col, scale=1.0)
+            else:
+                nc.gpsimd.tensor_scalar(out=out, in0=in_, scalar1=col, scalar2=1.0, op0=ALU.add, op1=ALU.mult)
+
+        def prepare(j, o, pt):
+            first = []
+            second = []
+            wide = o % 3 == 2
+            for q in range(NPAIR):
+                if wide and q == 1:
+                    continue
+                us = work.tile([P, ROWS], F32, name="us", tag="u")
+                gs = work.tile([P, ROWS], F32, name="gs", tag="u")
+                base = qa[:, j, o : o + 1] if wide and q == 0 else ta[:, j, q, o : o + 1]
+                step = qd[:, 0, j, o : o + 1] if wide and q == 0 else dt[:, j, q, o : o + 1]
+                nc.scalar.activation(out=gs[:], in_=pt[:, 2 * q + 1, :], func=ACT.Relu, bias=step, scale=1.0)
+                affine("S" if q == 3 and o % 3 == 0 else "G", us[:], pt[:, 2 * q, :], base)
+                first.append(us)
+                second.append(gs)
+            return first, second
+
+        def widen(j, o, banks, gs, piece):
+            k = piece // 2
+            cols = slice((piece % 2) * 512, (piece % 2 + 1) * 512)
+            nc.vector.scalar_tensor_tensor(
+                out=gs[:, cols],
+                in0=banks[piece][:].rearrange("p t n -> p (t n)"),
+                scalar=qd[:, k + 1, j, o : o + 1],
+                in1=gs[:, cols],
+                op0=ALU.add,
+                op1=ALU.max,
+            )
+
+        steps_of = {}
+        pts = {}
+        turned_of = {}
+        pts[0], steps_of[0], turned_of[0] = projection(0)
+        for step in steps_of[0]:
+            step()
+        banks = settle(turned_of[0])
+        ready = prepare(0, 0, pts[0])
+        ctx.enter_context(tc.manual_schedule())
+        for j in range(3):
             out_view = outs[j].rearrange("n (p s) o -> p n s o", s=2)
-            for oq in range(DK // OQ):
-                y = yp.tile([P, 4, H, 2, OQ], F32, name="y", tag="y")
-                for ol in range(OQ):
-                    o = oq * OQ + ol
-                    first = []
-                    second = []
-                    for q in range(NPAIR):
-                        if q < VPAIRS:
-                            gv = work.tile([P, ROWS], F32, name="gv", tag="gv%d" % q)
-                            nc.vector.tensor_scalar(
-                                out=gv[:],
-                                in0=pt[:, 2 * q + 1, :],
-                                scalar1=tl[:, j, 2 * q + 1, o : o + 1],
-                                scalar2=tl[:, j, 2 * q, o : o + 1],
-                                op0=ALU.add,
-                                op1=ALU.max,
-                            )
-                            first.append(pt[:, 2 * q, :])
-                            second.append(gv[:])
-                        else:
-                            us = work.tile([P, ROWS], F32, name="us", tag="us%d" % q)
-                            gs = work.tile([P, ROWS], F32, name="gs", tag="gs%d" % q)
-                            if q == VPAIRS:
-                                nc.scalar.activation(
-                                    out=us[:], in_=pt[:, 2 * q, :], func=ACT.Identity,
-                                    bias=ta[:, j, q - VPAIRS, o : o + 1], scale=1.0,
-                                )
-                            else:
-                                nc.gpsimd.tensor_scalar(
-                                    out=us[:], in0=pt[:, 2 * q, :],
-                                    scalar1=ta[:, j, q - VPAIRS, o : o + 1], scalar2=1.0,
-                                    op0=ALU.add, op1=ALU.mult,
-                                )
-                            nc.scalar.activation(
-                                out=gs[:], in_=pt[:, 2 * q + 1, :], func=ACT.Relu,
-                                bias=dt[:, j, q - VPAIRS, o : o + 1], scale=1.0,
-                            )
-                            first.append(us[:])
-                            second.append(gs[:])
-                    for t in range(8):
-                        ft = psum.tile([P, NPAIR, P], F32, name="ft", tag="bank")
-                        cols = slice(t * P, (t + 1) * P)
-                        for q in range(NPAIR):
-                            nc.tensor.matmul(
-                                out=ft[:, q, :], lhsT=first[q][:, cols], rhs=ident[:],
-                                start=True, stop=False, is_transpose=True,
-                            )
-                            nc.tensor.matmul(
-                                out=ft[:, q, :], lhsT=second[q][:, cols], rhs=ident[:],
-                                start=False, stop=True, is_transpose=True,
-                            )
-                        nc.vector.tensor_reduce(
-                            out=y[:, t // 2, :, t % 2, ol],
-                            in_=ft[:].rearrange("p q (h a) -> p h q a", a=CH),
-                            axis=mybir.AxisListType.XY,
-                            op=ALU.max,
+            if j < 2:
+                pts[j + 1], steps_of[j + 1], turned_of[j + 1] = projection(j + 1)
+            for o in range(DK):
+                oq, ol = divmod(o, OQ)
+                if ol == 0:
+                    y = yp.tile([P, 4, H, 2, OQ], F32, name="y", tag="y")
+                first, second = ready
+                nj, no = (j, o + 1) if o + 1 < DK else (j + 1, 0)
+                if nj < 3:
+                    ready = prepare(nj, no, pts[nj])
+                n_c = len(first)
+                for t in range(8):
+                    ft = psum.tile([P, n_c, P], F32, name="ft", tag="bank")
+                    cols = slice(t * P, (t + 1) * P)
+                    for q in range(n_c):
+                        nc.tensor.matmul(
+                            out=ft[:, q, :], lhsT=first[q][:, cols], rhs=ident[:],
+                            start=True, stop=False, is_transpose=True,
                         )
-                y_view = y[:].rearrange("p b h s o -> p (b h) s o")
-                for s in range(2):
-                    nc.sync.dma_start(out=out_view[:, :, s, oq * OQ : (oq + 1) * OQ], in_=y_view[:, :, s, :])
-
-        pts = [project(0, w_raws[0])]
-        w_raws.append(load_w(1))
-        pts.append(project(1, w_raws[1]))
-        tropical(0, pts[0])
-        w_raws.append(load_w(2))
-        pts.append(project(2, w_raws[2]))
-        tropical(1, pts[1])
-        tropical(2, pts[2])
+                        nc.tensor.matmul(
+                            out=ft[:, q, :], lhsT=second[q][:, cols], rhs=ident[:],
+                            start=False, stop=True, is_transpose=True,
+                        )
+                    nc.vector.tensor_reduce(
+                        out=y[:, t // 2, :, t % 2, ol],
+                        in_=ft[:].rearrange("p q (h a) -> p h q a", a=CH),
+                        axis=mybir.AxisListType.XY,
+                        op=ALU.max,
+                    )
+                    if nj == j and no % 3 == 2 and t % 2 == 1:
+                        widen(j, no, banks, ready[1][0], t // 2)
+                if j < 2 and o >= 3 and o % 3 == 0 and (o - 3) // 3 < len(steps_of[j + 1]):
+                    steps_of[j + 1][(o - 3) // 3]()
+                if ol == OQ - 1:
+                    y_view = y[:].rearrange("p b h s o -> p (b h) s o")
+                    for s in range(2):
+                        nc.sync.dma_start(out=out_view[:, :, s, oq * OQ : (oq + 1) * OQ], in_=y_view[:, :, s, :])
+                if o == DK - 1 and j < 2:
+                    banks = settle(turned_of[j + 1])

@@ -19,6 +19,9 @@ DK = 64
 CH = 8
 NPAIR = 4
 OQ = 16
+RING = 23
+WARM = 5
+WIDE = 2
 GAP = 128.0
 FLOOR = -3.0e38
 
@@ -38,25 +41,24 @@ def tile_tropicalattention_pa_kernel(
         xq = ctx.enter_context(tc.tile_pool(name="xq", bufs=1))
         wq = ctx.enter_context(tc.tile_pool(name="wq", bufs=1))
         pp = ctx.enter_context(tc.tile_pool(name="pp", bufs=2))
-        work = ctx.enter_context(tc.tile_pool(name="work", bufs=18))
-        rowp = ctx.enter_context(tc.tile_pool(name="rowp", bufs=1))
+        work = ctx.enter_context(tc.tile_pool(name="work", bufs=RING))
+        farp = ctx.enter_context(tc.tile_pool(name="farp", bufs=1))
         yp = ctx.enter_context(tc.tile_pool(name="yp", bufs=2))
-        psum = ctx.enter_context(tc.psum_pool(name="psum", bufs=4))
+        psum = ctx.enter_context(tc.psum_pool(name="psum", bufs=7))
         resid = ctx.enter_context(tc.psum_pool(name="resid", bufs=1))
+        ctx.enter_context(tc.manual_schedule())
 
         ident = const.tile([P, P], F32, name="ident")
         make_identity(nc, ident[:])
 
-        def load_halves(view, label):
-            halves = []
-            for half in range(2):
-                raw = rawp.tile([P, 4 * D], BF16, name="%s%d" % (label, half), tag="raw")
-                nc.sync.dma_start(out=raw[:], in_=view[:, half * 4 * D : (half + 1) * 4 * D])
-                halves.append(raw)
-            return halves
-
-        def load_w(j):
-            return load_halves(weights[j].rearrange("(m c) k -> m (c k)", c=CH), "w_raw")
+        t_a = const.tile([P, DK], BF16, name="t_a")
+        t_b = const.tile([P, DK], BF16, name="t_b")
+        nc.sync.dma_start(out=t_a[0:64, :], in_=Wq_trop)
+        nc.sync.dma_start(out=t_a[64:128, :], in_=Wk_trop)
+        nc.sync.dma_start(out=t_b[0:64, :], in_=Wv_trop)
+        nc.sync.dma_start(out=t_b[64:128, :], in_=Wv_trop)
+        lam_sb = const.tile([P, CH], BF16, name="lam_sb")
+        nc.sync.dma_start(out=lam_sb[:], in_=lam.rearrange("a b (m c) -> (a b m) c", c=CH))
 
         x_raw = []
         x_view = x.rearrange("b (p s) k -> p b (s k)", s=2)
@@ -65,259 +67,347 @@ def tile_tropicalattention_pa_kernel(
             nc.sync.dma_start(
                 out=raw[:].rearrange("p (b f) -> p b f", b=2), in_=x_view[:, 2 * half : 2 * half + 2, :]
             )
-            x_raw.append(raw)
+            x_raw.append(raw[:])
 
-        t_a = const.tile([P, DK], BF16, name="t_a")
-        t_b = const.tile([P, DK], BF16, name="t_b")
-        nc.scalar.dma_start(out=t_a[0:64, :], in_=Wq_trop)
-        nc.scalar.dma_start(out=t_a[64:128, :], in_=Wk_trop)
-        nc.scalar.dma_start(out=t_b[0:64, :], in_=Wv_trop)
-        nc.scalar.dma_start(out=t_b[64:128, :], in_=Wv_trop)
-        lam_sb = const.tile([P, CH], BF16, name="lam_sb")
-        nc.scalar.dma_start(out=lam_sb[:], in_=lam.rearrange("a b (m c) -> (a b m) c", c=CH))
+        def load_w(j):
+            view = weights[j].rearrange("(m c) k -> m (c k)", c=CH)
+            if j == 0:
+                both = pp.tile([P, 8 * D], BF16, name="w_raw", tag="pt")
+                halves = [both[:, 0 : 4 * D], both[:, 4 * D : 8 * D]]
+            else:
+                halves = [rawp.tile([P, 4 * D], BF16, name="w_raw%d" % h, tag="raw")[:] for h in range(2)]
+            for half in range(2):
+                nc.sync.dma_start(out=halves[half], in_=view[:, half * 4 * D : (half + 1) * 4 * D])
+            return halves
 
-        def quantise_part(raws, codes, scales, use_vector, half, g):
-            rawf = raws[half][:].bitcast(F32)
-            grouped = grp.tile([P, 2048], BF16, name="grouped", tag="grouped", align_bytes=64)
+        def turn_words(raws, half, g, pair):
+            rawf = raws[half].bitcast(F32)
+            tp = psum.tile([P, 2, 2, P], F32, name="tp", tag="bank")
+            for tt in range(2):
+                for u in range(2):
+                    col = (2 * pair + tt) * 512 + 256 * g + 128 * u
+                    nc.tensor.transpose(tp[:, tt, u, :], rawf[:, col : col + P], ident[:])
+            return tp
+
+        def group_words(grouped, tp, pair, copy):
             gf = grouped[:].bitcast(F32)
-            for pair in range(2):
-                tp = psum.tile([P, 2, 2, P], F32, name="tp", tag="bank")
-                for tt in range(2):
-                    for u in range(2):
-                        col = (2 * pair + tt) * 512 + 256 * g + 128 * u
-                        nc.tensor.transpose(tp[:, tt, u, :], rawf[:, col : col + P], ident[:])
-                dst = gf[:, pair * 512 : (pair + 1) * 512].rearrange("q (t n u) -> q t n u", t=2, u=2)
-                src = tp[:].rearrange("q t u n -> q t n u")
-                if use_vector and pair == 0:
-                    nc.vector.tensor_copy(out=dst, in_=src)
-                else:
-                    nc.scalar.copy(out=dst, in_=src)
+            copy(
+                out=gf[:, pair * 512 : (pair + 1) * 512].rearrange("q (t n u) -> q t n u", t=2, u=2),
+                in_=tp[:].rearrange("q t u n -> q t n u"),
+            )
+
+        def new_grouped():
+            return grp.tile([P, 2048], BF16, name="grouped", tag="grouped", align_bytes=64)
+
+        def quantise(grouped, codes, scales, half, g):
             nc.vector.quantize_mx(
                 out=codes[g][:, half * 512 : (half + 1) * 512].bitcast(FP8X4),
                 scales=scales[g][:, half * 512 : (half + 1) * 512],
                 in_=grouped[:],
             )
 
-        x_codes = [xq.tile([P, ROWS], U32, name="x_codes%d" % g, align_bytes=64) for g in range(2)]
-        x_scales = [xq.tile([P, ROWS], U8, name="x_scales%d" % g, align_bytes=64) for g in range(2)]
-        for half in range(2):
-            for g in range(2):
-                quantise_part(x_raw, x_codes, x_scales, True, half, g)
+        def group_quarter(raws, half, g):
+            grouped = new_grouped()
+            for pair in range(2):
+                group_words(grouped, turn_words(raws, half, g, pair), pair, nc.scalar.copy)
+            return grouped
+
+        w_raw0 = load_w(0)
 
         lam_f = const.tile([P, CH], F32, name="lam_f")
         nc.vector.tensor_copy(out=lam_f[:], in_=lam_sb[:])
         tl = const.tile([P, 3, CH, DK], F32, name="tl")
-        for which, t_sb in enumerate([t_a, t_b]):
-            rep = const.tile([P, CH, H, CH], F32, name="rep", tag="rep")
+        reps = []
+        for t_sb in (t_a, t_b):
+            rep = work.tile([P, CH, H, CH], F32, name="rep", tag="u")
             nc.vector.tensor_copy(
                 out=rep[:],
                 in_=t_sb[:].rearrange("p (a c) -> p c a", c=CH).unsqueeze(2).to_broadcast([P, CH, H, CH]),
             )
+            reps.append(rep)
+        for which in range(2):
             for quad in range(2):
                 tq = psum.tile([P, 4, P], F32, name="tq", tag="bank")
                 for cc in range(4):
-                    c = 4 * quad + cc
-                    nc.tensor.transpose(tq[:, cc, :], rep[:, c, :, :].rearrange("p h a -> p (h a)"), ident[:])
+                    nc.tensor.transpose(
+                        tq[:, cc, :], reps[which][:, 4 * quad + cc, :, :].rearrange("p h a -> p (h a)"), ident[:]
+                    )
                 for cc in range(4):
                     c = 4 * quad + cc
                     if which == 0:
-                        nc.vector.tensor_scalar(
-                            out=tl[:, 0:2, c, :],
-                            in0=tq[:, cc, :].rearrange("p (j o) -> p j o", j=2),
-                            scalar1=lam_f[:, c : c + 1],
-                            scalar2=None,
-                            op0=ALU.subtract,
-                        )
+                        out = tl[:, 0:2, c, :]
+                        in0 = tq[:, cc, :].rearrange("p (j o) -> p j o", j=2)
                     else:
-                        nc.vector.tensor_scalar(
-                            out=tl[:, 2, c, :],
-                            in0=tq[:, cc, 0:DK],
-                            scalar1=lam_f[:, c : c + 1],
-                            scalar2=None,
-                            op0=ALU.subtract,
-                        )
-        fl = const.tile([P, 3, CH, DK], F32, name="fl")
-        nc.vector.tensor_scalar_max(
-            out=fl[:].rearrange("p j c o -> p (j c o)"), in0=tl[:].rearrange("p j c o -> p (j c o)"), scalar1=FLOOR
-        )
-        ta = const.tile([P, 3, NPAIR, DK], F32, name="ta")
-        dt = const.tile([P, 3, NPAIR, DK], F32, name="dt")
-        for j in range(3):
-            even = fl[:, j, :, :].rearrange("p (q e) o -> p q e o", e=2)[:, :, 0, :]
-            odd = fl[:, j, :, :].rearrange("p (q e) o -> p q e o", e=2)[:, :, 1, :]
-            nc.vector.scalar_tensor_tensor(
-                out=ta[:, j, :, :], in0=odd, scalar=-GAP, in1=even, op0=ALU.add, op1=ALU.max
-            )
-            nc.vector.scalar_tensor_tensor(
-                out=dt[:, j, :, :], in0=even, scalar=-GAP, in1=odd, op0=ALU.add, op1=ALU.max
-            )
-        nc.vector.tensor_tensor(out=dt[:], in0=dt[:], in1=ta[:], op=ALU.subtract)
-        top = const.tile([P, 3, DK], F32, name="top")
-        nc.vector.tensor_tensor(out=top[:], in0=fl[:, :, 0, :], in1=fl[:, :, 1, :], op=ALU.max)
-        for c in (2, 3):
-            nc.vector.tensor_tensor(out=top[:], in0=top[:], in1=fl[:, :, c, :], op=ALU.max)
-        qa = const.tile([P, 3, DK], F32, name="qa")
-        qd = const.tile([P, 3, 3, DK], F32, name="qd")
-        nc.vector.scalar_tensor_tensor(
-            out=qa[:], in0=top[:], scalar=-GAP, in1=fl[:, :, 0, :], op0=ALU.add, op1=ALU.max
-        )
-        for c in (1, 2, 3):
-            nc.vector.scalar_tensor_tensor(
-                out=qd[:, c - 1, :, :], in0=top[:], scalar=-GAP, in1=fl[:, :, c, :], op0=ALU.add, op1=ALU.max
-            )
-            nc.vector.tensor_tensor(
-                out=qd[:, c - 1, :, :], in0=qd[:, c - 1, :, :], in1=qa[:], op=ALU.subtract
-            )
-
-        def projection(j):
-            w_codes = [wq.tile([P, ROWS], U32, name="w_codes%d" % g, align_bytes=64) for g in range(2)]
-            w_scales = [wq.tile([P, ROWS], U8, name="w_scales%d" % g, align_bytes=64) for g in range(2)]
-            pt = pp.tile([P, CH, ROWS], F32, name="pt", tag="pt")
-            raws = load_w(j)
-            steps = []
-
-            def diff_engine():
-                return nc.vector if j == 0 else nc.gpsimd
-
-            def chunk(c):
-                for rh in range(2):
-                    z = psum.tile([P, 512], F32, name="z", tag="bank")
-                    for g in range(2):
-                        nc.tensor.matmul_mx(
-                            out=z[:],
-                            lhsT=w_codes[g][:, c * P : (c + 1) * P].bitcast(FP8X4),
-                            lhsT_scale=w_scales[g][:, c * P : (c + 1) * P],
-                            rhs=x_codes[g][:, rh * 512 : (rh + 1) * 512].bitcast(FP8X4),
-                            rhs_scale=x_scales[g][:, rh * 512 : (rh + 1) * 512],
-                            start=(g == 0),
-                            stop=(g == 1),
-                        )
-                    dst = pt[:, c, rh * 512 : (rh + 1) * 512]
-                    if j == 0:
-                        nc.vector.tensor_scalar_max(out=dst, in0=z[:], scalar1=0.0)
-                    else:
-                        nc.scalar.activation(out=dst, in_=z[:], func=ACT.Relu)
-                nc.scalar.activation(out=pt[:, c, :], in_=pt[:, c, :], func=ACT.Ln, bias=1.0, scale=1.0)
-                if c in (2, 3):
-                    tmp = work.tile([P, ROWS], F32, name="tmp", tag="u")
-                    diff_engine().tensor_tensor(out=tmp[:], in0=pt[:, c, :], in1=pt[:, 0, :], op=ALU.subtract)
-                    turn(c - 2, tmp)
-                if c % 2 == 1:
-                    diff_engine().tensor_tensor(out=pt[:, c, :], in0=pt[:, c, :], in1=pt[:, c - 1, :], op=ALU.subtract)
-
-            def turn(k, tmp):
-                rows = rowp.tile([P, ROWS], F32, name="rows", tag="rows%d" % k)
-                for half in range(2):
-                    bank = psum.tile([P, 4, P], F32, name="tr", tag="bank")
-                    for t in range(4):
-                        col = (4 * half + t) * P
-                        nc.tensor.transpose(bank[:, t, :], tmp[:, col : col + P], ident[:])
-                    nc.scalar.copy(out=rows[:, half * 512 : (half + 1) * 512], in_=bank[:].rearrange("p t n -> p (t n)"))
-                turned.append(rows)
-
-            turned = []
-            for half in range(2):
-                for g in range(2):
-                    steps.append(
-                        lambda half=half, g=g: quantise_part(raws, w_codes, w_scales, j == 0, half, g)
+                        out = tl[:, 2, c, :]
+                        in0 = tq[:, cc, 0:DK]
+                    nc.vector.tensor_scalar(
+                        out=out, in0=in0, scalar1=lam_f[:, c : c + 1], scalar2=FLOOR, op0=ALU.subtract, op1=ALU.max
                     )
-            for c in range(CH):
-                steps.append(lambda c=c: chunk(c))
-            return pt, steps, turned
 
-        def settle(turned):
-            banks = []
-            for k in range(2):
-                for half in range(2):
-                    bank = resid.tile([P, 4, P], F32, name="far%d%d" % (k, half), tag="far%d%d" % (k, half))
-                    for t in range(4):
-                        col = (4 * half + t) * P
-                        nc.tensor.transpose(bank[:, t, :], turned[k][:, col : col + P], ident[:])
-                    banks.append(bank)
-            return banks
+        top4 = const.tile([P, 3, 4, DK], F32, name="top4")
+        dt = const.tile([P, 3, NPAIR, DK], F32, name="dt")
+        qd = const.tile([P, 2, 3, DK], F32, name="qd")
 
-        def affine(eng, out, in_, col):
-            if eng == "S":
-                nc.scalar.activation(out=out, in_=in_, func=ACT.Identity, bias=col, scale=1.0)
-            else:
-                nc.gpsimd.tensor_scalar(out=out, in0=in_, scalar1=col, scalar2=1.0, op0=ALU.add, op1=ALU.mult)
+        def highest(out, in0, in1):
+            nc.vector.tensor_tensor(out=out, in0=in0, in1=in1, op=ALU.max)
 
-        def prepare(j, o, pt):
-            first = []
-            second = []
-            wide = o % 3 == 2
-            for q in range(NPAIR):
-                if wide and q == 1:
-                    continue
-                us = work.tile([P, ROWS], F32, name="us", tag="u")
-                gs = work.tile([P, ROWS], F32, name="gs", tag="u")
-                base = qa[:, j, o : o + 1] if wide and q == 0 else ta[:, j, q, o : o + 1]
-                step = qd[:, 0, j, o : o + 1] if wide and q == 0 else dt[:, j, q, o : o + 1]
-                nc.scalar.activation(out=gs[:], in_=pt[:, 2 * q + 1, :], func=ACT.Relu, bias=step, scale=1.0)
-                affine("S" if q == 3 and o % 3 == 0 else "G", us[:], pt[:, 2 * q, :], base)
-                first.append(us)
-                second.append(gs)
-            return first, second
+        def less(out, in0, in1):
+            nc.vector.tensor_tensor(out=out, in0=in0, in1=in1, op=ALU.subtract)
 
-        def widen(j, o, banks, gs, piece):
-            k = piece // 2
-            cols = slice((piece % 2) * 512, (piece % 2 + 1) * 512)
+        def raise_low(j):
             nc.vector.scalar_tensor_tensor(
-                out=gs[:, cols],
-                in0=banks[piece][:].rearrange("p t n -> p (t n)"),
-                scalar=qd[:, k + 1, j, o : o + 1],
-                in1=gs[:, cols],
+                out=tl[:, j, :, :],
+                in0=top4[:, j, 0, :].unsqueeze(1).to_broadcast([P, CH, DK]),
+                scalar=-GAP,
+                in1=tl[:, j, :, :],
                 op0=ALU.add,
                 op1=ALU.max,
             )
 
-        steps_of = {}
-        pts = {}
-        turned_of = {}
-        pts[0], steps_of[0], turned_of[0] = projection(0)
-        for step in steps_of[0]:
-            step()
-        banks = settle(turned_of[0])
-        ready = prepare(0, 0, pts[0])
-        ctx.enter_context(tc.manual_schedule())
+        pairs = tl[:].rearrange("p j (q e) o -> p (j q) e o", e=2)
+        table_steps = [
+            lambda: highest(top4[:], tl[:, :, 0:4, :], tl[:, :, 4:8, :]),
+            lambda: highest(top4[:, :, 0:2, :], top4[:, :, 0:2, :], top4[:, :, 2:4, :]),
+            lambda: highest(top4[:, :, 0, :], top4[:, :, 0, :], top4[:, :, 1, :]),
+            lambda: raise_low(0),
+            lambda: raise_low(1),
+            lambda: raise_low(2),
+            lambda: less(dt[:].rearrange("p j q o -> p (j q) o"), pairs[:, :, 1, :], pairs[:, :, 0, :]),
+            lambda: [less(qd[:, k, :, :], tl[:, :, 2 + k, :], tl[:, :, 0, :]) for k in range(2)],
+        ]
+
+        x_codes = [xq.tile([P, ROWS], U32, name="x_codes%d" % g, align_bytes=64) for g in range(2)]
+        x_scales = [xq.tile([P, ROWS], U8, name="x_scales%d" % g, align_bytes=64) for g in range(2)]
+        for half in range(2):
+            for g in range(2):
+                quantise(group_quarter(x_raw, half, g), x_codes, x_scales, half, g)
+                table_steps.pop(0)()
+
+        def new_w():
+            codes = [wq.tile([P, ROWS], U32, name="w_codes%d" % g, align_bytes=64) for g in range(2)]
+            scales = [wq.tile([P, ROWS], U8, name="w_scales%d" % g, align_bytes=64) for g in range(2)]
+            return codes, scales
+
+        def new_p():
+            return pp.tile([P, CH, ROWS], F32, name="pt", tag="pt")
+
+        def multiply(w, c, rh):
+            codes, scales = w
+            z = psum.tile([P, 512], F32, name="z", tag="bank")
+            for g in range(2):
+                nc.tensor.matmul_mx(
+                    out=z[:],
+                    lhsT=codes[g][:, c * P : (c + 1) * P].bitcast(FP8X4),
+                    lhsT_scale=scales[g][:, c * P : (c + 1) * P],
+                    rhs=x_codes[g][:, rh * 512 : (rh + 1) * 512].bitcast(FP8X4),
+                    rhs_scale=x_scales[g][:, rh * 512 : (rh + 1) * 512],
+                    start=(g == 0),
+                    stop=(g == 1),
+                )
+            return z
+
+        def relu_v(pt, c, rh, z):
+            nc.vector.tensor_scalar_max(out=pt[:, c, rh * 512 : (rh + 1) * 512], in0=z[:], scalar1=0.0)
+
+        def log(pt, c, cols):
+            nc.scalar.activation(out=pt[:, c, cols], in_=pt[:, c, cols], func=ACT.Ln, bias=1.0, scale=1.0)
+
+        def odd_difference(eng, pt, c):
+            eng.tensor_tensor(out=pt[:, c, :], in0=pt[:, c, :], in1=pt[:, c - 1, :], op=ALU.subtract)
+
+        WR = WIDE * P
+
+        def far_differences(eng, pt):
+            far = farp.tile([P, 2, WR], F32, name="far", tag="far")
+            eng.tensor_tensor(out=far[:, 0, :], in0=pt[:, 2, 0:WR], in1=pt[:, 0, 0:WR], op=ALU.subtract)
+            eng.tensor_tensor(out=far[:, 1, :], in0=pt[:, 3, 0:WR], in1=far[:, 0, :], op=ALU.add)
+            return far
+
+        def turn_far(far, copy):
+            turned = farp.tile([P, 2, WIDE, P], F32, name="turned", tag="turned")
+            for k in range(2):
+                bank = psum.tile([P, WIDE, P], F32, name="tr", tag="bank")
+                for t in range(WIDE):
+                    nc.tensor.transpose(bank[:, t, :], far[:, k, t * P : (t + 1) * P], ident[:])
+                copy(out=turned[:, k, :, :], in_=bank[:])
+            return turned
+
+        def settle(turned):
+            bank = resid.tile([P, 2, WR], F32, name="settled", tag="settled")
+            for k in range(2):
+                for t in range(WIDE):
+                    nc.tensor.transpose(bank[:, k, t * P : (t + 1) * P], turned[:, k, t, :], ident[:])
+            return bank
+
+        def relu_part(out, in_, step):
+            nc.scalar.activation(out=out, in_=in_, func=ACT.Relu, bias=step, scale=1.0)
+
+        def base_part(on_scalar, out, in_, col):
+            if on_scalar:
+                nc.scalar.activation(out=out, in_=in_, func=ACT.Identity, bias=col, scale=1.0)
+            else:
+                nc.gpsimd.tensor_scalar(out=out, in0=in_, scalar1=col, scalar2=1.0, op0=ALU.add, op1=ALU.mult)
+
+        def base_of(j, o, pt, us, q):
+            lo = WR if q == 1 else 0
+            base_part(q == 1 and o % 4 != 0, us[:, lo:ROWS], pt[:, 2 * q, lo:ROWS], tl[:, j, 2 * q, o : o + 1])
+
+        def relu_of(j, o, pt, gs, q):
+            lo = WR if q == 1 else 0
+            relu_part(gs[:, lo:ROWS], pt[:, 2 * q + 1, lo:ROWS], dt[:, j, q, o : o + 1])
+
+        def prepare(j, o, pt):
+            first = []
+            second = []
+            for q in range(NPAIR):
+                us = work.tile([P, ROWS], F32, name="us", tag="u")
+                gs = work.tile([P, ROWS], F32, name="gs", tag="u")
+                relu_of(j, o, pt, gs, q)
+                base_of(j, o, pt, us, q)
+                first.append(us)
+                second.append(gs)
+            return first, second
+
+        def widen(j, o, settled, gs, k):
+            nc.vector.scalar_tensor_tensor(
+                out=gs[:, 0:WR],
+                in0=settled[:, k, :],
+                scalar=qd[:, k, j, o : o + 1],
+                in1=gs[:, 0:WR],
+                op0=ALU.add,
+                op1=ALU.max,
+            )
+
+        w = new_w()
+        pt = new_p()
+        quarters = [(half, g) for half in range(2) for g in range(2)]
+
+        def quantise_w0(n):
+            half, g = quarters[n]
+            quantise(group_quarter(w_raw0, half, g), w[0], w[1], half, g)
+            table_steps.pop(0)()
+
+        def chunk0(c):
+            zs = [multiply(w, c, rh) for rh in range(2)]
+            for rh in range(2):
+                relu_v(pt, c, rh, zs[rh])
+
+        for n in range(3):
+            quantise_w0(n)
+        chunk0(0)
+        quantise_w0(3)
+        chunk0(1)
+        log(pt, 0, slice(0, ROWS))
+        first = []
+        second = []
+        for c in range(1, CH):
+            if c + 1 < CH:
+                chunk0(c + 1)
+            log(pt, c, slice(0, ROWS))
+            if c == 6:
+                odd_difference(nc.vector, pt, 5)
+            if c % 2 == 1:
+                q = c // 2
+                us = work.tile([P, ROWS], F32, name="us", tag="u")
+                gs = work.tile([P, ROWS], F32, name="gs", tag="u")
+                base_of(0, 0, pt, us, q)
+                if q < 2:
+                    odd_difference(nc.gpsimd, pt, c)
+                first.append(us)
+                second.append(gs)
+            elif c > 2:
+                relu_of(0, 0, pt, second[c // 2 - 2], c // 2 - 2)
+        odd_difference(nc.vector, pt, 7)
+        for q in range(2, NPAIR):
+            relu_of(0, 0, pt, second[q], q)
+        settled = settle(turn_far(far_differences(nc.vector, pt), nc.vector.tensor_copy))
+        warm = const.tile([P, 512], BF16, name="warm")
+        nc.vector.tensor_copy(out=warm[:], in_=second[2][:, 0:512])
+        bank = psum.tile([P, 512], F32, name="warm_bank", tag="bank")
+        for k in range(WARM):
+            nc.tensor.matmul(out=bank[:], lhsT=warm[:, 0:P], rhs=warm[:], start=True, stop=True)
+        ready = [(first, second), prepare(0, 1, pt)]
+        for o in range(2):
+            for k in range(2):
+                widen(0, o, settled, ready[o][1][0], k)
+
         for j in range(3):
             out_view = outs[j].rearrange("n (p s) o -> p n s o", s=2)
             if j < 2:
-                pts[j + 1], steps_of[j + 1], turned_of[j + 1] = projection(j + 1)
+                w_raw = load_w(j + 1)
+                w_next = new_w()
+                next_p = new_p()
+            grouped = None
+            z = None
+            logs = []
             for o in range(DK):
                 oq, ol = divmod(o, OQ)
                 if ol == 0:
-                    y = yp.tile([P, 4, H, 2, OQ], F32, name="y", tag="y")
-                first, second = ready
-                nj, no = (j, o + 1) if o + 1 < DK else (j + 1, 0)
+                    y = yp.tile([P, 2, 4, H, OQ], F32, name="y", tag="y")
+                first, second = ready.pop(0)
+                nj, no = (j, o + 2) if o + 2 < DK else (j + 1, o + 2 - DK)
                 if nj < 3:
-                    ready = prepare(nj, no, pts[nj])
-                n_c = len(first)
+                    ready.append(prepare(nj, no, pt if nj == j else next_p))
+                for c, rh in logs:
+                    log(next_p, c, slice(rh * 512, (rh + 1) * 512))
+                    if c % 2 == 1 and rh == 1:
+                        odd_difference(nc.gpsimd, next_p, c)
+                    if c == 3 and rh == 1:
+                        far = far_differences(nc.gpsimd, next_p)
+                logs = []
                 for t in range(8):
-                    ft = psum.tile([P, n_c, P], F32, name="ft", tag="bank")
+                    if no == 0 and nj < 3 and t == 3:
+                        settled = settle(turned)
+                    used = [0, 2, 3] if t < WIDE else [0, 1, 2, 3]
+                    ft = psum.tile([P, len(used), P], F32, name="ft", tag="bank")
                     cols = slice(t * P, (t + 1) * P)
-                    for q in range(n_c):
+                    for n, q in enumerate(used):
                         nc.tensor.matmul(
-                            out=ft[:, q, :], lhsT=first[q][:, cols], rhs=ident[:],
+                            out=ft[:, n, :], lhsT=first[q][:, cols], rhs=ident[:],
                             start=True, stop=False, is_transpose=True,
                         )
                         nc.tensor.matmul(
-                            out=ft[:, q, :], lhsT=second[q][:, cols], rhs=ident[:],
+                            out=ft[:, n, :], lhsT=second[q][:, cols], rhs=ident[:],
                             start=False, stop=True, is_transpose=True,
                         )
                     nc.vector.tensor_reduce(
-                        out=y[:, t // 2, :, t % 2, ol],
+                        out=y[:, t % 2, t // 2, :, ol],
                         in_=ft[:].rearrange("p q (h a) -> p h q a", a=CH),
                         axis=mybir.AxisListType.XY,
                         op=ALU.max,
                     )
-                    if nj == j and no % 3 == 2 and t % 2 == 1:
-                        widen(j, no, banks, ready[1][0], t // 2)
-                if j < 2 and o >= 3 and o % 3 == 0 and (o - 3) // 3 < len(steps_of[j + 1]):
-                    steps_of[j + 1][(o - 3) // 3]()
-                if ol == OQ - 1:
-                    y_view = y[:].rearrange("p b h s o -> p (b h) s o")
+                    if nj < 3 and t in (5, 7):
+                        widen(nj, no, settled, ready[1][1][0], (t - 5) // 2)
+                    if j == 2 and o == DK - 1 and t % 2 == 1:
+                        b = t // 2
+                        for s in range(2):
+                            nc.sync.dma_start(
+                                out=out_view[:, H * b : H * (b + 1), s, oq * OQ : (oq + 1) * OQ], in_=y[:, s, b, :, :]
+                            )
+                    if j < 2:
+                        if 1 <= o < 9:
+                            part_no, pair = divmod(o - 1, 2)
+                            half, g = divmod(part_no, 2)
+                            if t == 3:
+                                tp = turn_words(w_raw, half, g, pair)
+                            if t == 4:
+                                if pair == 0:
+                                    grouped = new_grouped()
+                                group_words(grouped, tp, pair, nc.vector.tensor_copy)
+                            if t == 6 and pair == 1:
+                                quantise(grouped, w_next[0], w_next[1], half, g)
+                        elif 9 <= o < 25:
+                            c, rh = divmod(o - 9, 2)
+                            if t == 3:
+                                z = multiply(w_next, c, rh)
+                            if t == 4:
+                                relu_v(next_p, c, rh, z)
+                                logs.append((c, rh))
+                        elif o == 30 and t == 3:
+                            turned = turn_far(far, nc.vector.tensor_copy)
+                if ol == OQ - 1 and not (j == 2 and o == DK - 1):
+                    y_view = y[:].rearrange("p s b h o -> p s (b h) o")
                     for s in range(2):
-                        nc.sync.dma_start(out=out_view[:, :, s, oq * OQ : (oq + 1) * OQ], in_=y_view[:, :, s, :])
-                if o == DK - 1 and j < 2:
-                    banks = settle(turned_of[j + 1])
+                        nc.sync.dma_start(out=out_view[:, :, s, oq * OQ : (oq + 1) * OQ], in_=y_view[:, s, :, :])
+            if j < 2:
+                pt = next_p

@@ -331,10 +331,12 @@ def tile_tropicalattention_pa_kernel(
             for k in range(2):
                 widen(0, o, settled, ready[o][1][0], k)
 
+        w_raws = {1: load_w(1)}
+
         for j in range(3):
             out_view = outs[j].rearrange("n (p s) o -> p n s o", s=2)
             if j < 2:
-                w_raw = load_w(j + 1)
+                w_raw = w_raws[j + 1]
                 w_next = new_w()
                 next_p = new_p()
             grouped = None
@@ -403,6 +405,8 @@ def tile_tropicalattention_pa_kernel(
                             if t == 4:
                                 relu_v(next_p, c, rh, z)
                                 logs.append((c, rh))
+                        elif o == 26 and t == 0 and j == 0:
+                            w_raws[2] = load_w(2)
                         elif o == 30 and t == 3:
                             turned = turn_far(far, nc.vector.tensor_copy)
                 if ol == OQ - 1 and not (j == 2 and o == DK - 1):

@@ -173,7 +173,7 @@ def tile_tropicalattention_pa_kernel(
             lambda: raise_low(1),
             lambda: raise_low(2),
             lambda: less(dt[:].rearrange("p j q o -> p (j q) o"), pairs[:, :, 1, :], pairs[:, :, 0, :]),
-            lambda: [less(qd[:, k, :, :], tl[:, :, 2 + k, :], tl[:, :, 0, :]) for k in range(2)],
+            lambda: [less(qd[:, k, :, :], tl[:, :, 2 * k, :], tl[:, :, 2 + k, :]) for k in range(2)],
         ]
 
         x_codes = [xq.tile([P, ROWS], U32, name="x_codes%d" % g, align_bytes=64) for g in range(2)]
@@ -249,8 +249,10 @@ def tile_tropicalattention_pa_kernel(
                 nc.gpsimd.tensor_scalar(out=out, in0=in_, scalar1=col, scalar2=1.0, op0=ALU.add, op1=ALU.mult)
 
         def base_of(j, o, pt, us, q):
-            lo = WR if q == 1 else 0
-            base_part(q == 1 and o % 4 != 0, us[:, lo:ROWS], pt[:, 2 * q, lo:ROWS], tl[:, j, 2 * q, o : o + 1])
+            lo = WR if q < 2 else 0
+            base_part(q == 1 and o % 3 == 1, us[:, lo:ROWS], pt[:, 2 * q, lo:ROWS], tl[:, j, 2 * q, o : o + 1])
+            if q == 0:
+                base_part(True, us[:, 0:WR], pt[:, 0, 0:WR], tl[:, j, 3, o : o + 1])
 
         def relu_of(j, o, pt, gs, q):
             lo = WR if q == 1 else 0
@@ -271,9 +273,9 @@ def tile_tropicalattention_pa_kernel(
         def widen(j, o, settled, gs, k):
             nc.vector.scalar_tensor_tensor(
                 out=gs[:, 0:WR],
-                in0=settled[:, k, :],
+                in0=gs[:, 0:WR],
                 scalar=qd[:, k, j, o : o + 1],
-                in1=gs[:, 0:WR],
+                in1=settled[:, k, :],
                 op0=ALU.add,
                 op1=ALU.max,
             )

@@ -389,27 +389,28 @@ def tile_tropicalattention_pa_kernel(
                                 out=out_view[:, H * b : H * (b + 1), s, oq * OQ : (oq + 1) * OQ], in_=y[:, s, b, :, :]
                             )
                     if j < 2:
-                        if 1 <= o < 9:
-                            part_no, pair = divmod(o - 1, 2)
-                            half, g = divmod(part_no, 2)
-                            if t == 3:
+                        if 1 <= o < 17:
+                            eighth, late = divmod(o - 1, 2)
+                            quarter, pair = divmod(eighth, 2)
+                            half, g = divmod(quarter, 2)
+                            if late == 0 and t == 3:
                                 tp = turn_words(w_raw, half, g, pair)
-                            if t == 4:
+                            if late == 0 and t == 4:
                                 if pair == 0:
                                     grouped = new_grouped()
                                 group_words(grouped, tp, pair, nc.vector.tensor_copy)
-                            if t == 6 and pair == 1:
+                            if late == 1 and pair == 1 and t == 3:
                                 quantise(grouped, w_next[0], w_next[1], half, g)
-                        elif 9 <= o < 25:
-                            c, rh = divmod(o - 9, 2)
+                        elif 17 <= o < 33:
+                            c, rh = divmod(o - 17, 2)
                             if t == 3:
                                 z = multiply(w_next, c, rh)
                             if t == 4:
                                 relu_v(next_p, c, rh, z)
                                 logs.append((c, rh))
-                        elif o == 26 and t == 0 and j == 0:
+                        elif o == 34 and t == 0 and j == 0:
                             w_raws[2] = load_w(2)
-                        elif o == 30 and t == 3:
+                        elif o == 38 and t == 3:
                             turned = turn_far(far, nc.vector.tensor_copy)
                 if ol == OQ - 1 and not (j == 2 and o == DK - 1):
                     y_view = y[:].rearrange("p s b h o -> p s (b h) o")

@@ -359,11 +359,13 @@ def tile_tropicalattention_pa_kernel(
                     if c == 3 and rh == 1:
                         far = far_differences(nc.gpsimd, next_p)
                 logs = []
+                blocks = []
                 for t in range(8):
                     if no == 0 and nj < 3 and t == 3:
                         settled = settle(turned)
                     used = [0, 2, 3] if t < WIDE else [0, 1, 2, 3]
                     ft = psum.tile([P, len(used), P], F32, name="ft", tag="bank")
+                    blocks.append((t, ft))
                     cols = slice(t * P, (t + 1) * P)
                     for n, q in enumerate(used):
                         nc.tensor.matmul(
@@ -374,12 +376,15 @@ def tile_tropicalattention_pa_kernel(
                             out=ft[:, n, :], lhsT=second[q][:, cols], rhs=ident[:],
                             start=False, stop=True, is_transpose=True,
                         )
-                    nc.vector.tensor_reduce(
-                        out=y[:, t % 2, t // 2, :, ol],
-                        in_=ft[:].rearrange("p q (h a) -> p h q a", a=CH),
-                        axis=mybir.AxisListType.XY,
-                        op=ALU.max,
-                    )
+                    if t % 2 == 1:
+                        for tb, fb in reversed(blocks):
+                            nc.vector.tensor_reduce(
+                                out=y[:, tb % 2, tb // 2, :, ol],
+                                in_=fb[:].rearrange("p q (h a) -> p h q a", a=CH),
+                                axis=mybir.AxisListType.XY,
+                                op=ALU.max,
+                            )
+                        blocks = []
                     if nj < 3 and t in (5, 7):
                         widen(nj, no, settled, ready[1][1][0], (t - 5) // 2)
                     if j == 2 and o == DK - 1 and t % 2 == 1:
@@ -393,9 +398,9 @@ def tile_tropicalattention_pa_kernel(
                             eighth, late = divmod(o - 1, 2)
                             quarter, pair = divmod(eighth, 2)
                             half, g = divmod(quarter, 2)
-                            if late == 0 and t == 3:
-                                tp = turn_words(w_raw, half, g, pair)
                             if late == 0 and t == 4:
+                                tp = turn_words(w_raw, half, g, pair)
+                            if late == 0 and t == 5:
                                 if pair == 0:
                                     grouped = new_grouped()
                                 group_words(grouped, tp, pair, nc.vector.tensor_copy)
@@ -403,9 +408,9 @@ def tile_tropicalattention_pa_kernel(
                                 quantise(grouped, w_next[0], w_next[1], half, g)
                         elif 17 <= o < 33:
                             c, rh = divmod(o - 17, 2)
-                            if t == 3:
-                                z = multiply(w_next, c, rh)
                             if t == 4:
+                                z = multiply(w_next, c, rh)
+                            if t == 5:
                                 relu_v(next_p, c, rh, z)
                                 logs.append((c, rh))
                         elif o == 34 and t == 0 and j == 0:

from contextlib import ExitStack

import concourse.mybir as mybir
from concourse.masks import make_identity

F32 = mybir.dt.float32
BF16 = mybir.dt.bfloat16
U32 = mybir.dt.uint32
U8 = mybir.dt.uint8
FP8X4 = mybir.dt.float8_e4m3fn_x4
ALU = mybir.AluOpType
ACT = mybir.ActivationFunctionType

P = 128
ROWS = 1024
D = 1024
H = 16
DK = 64
CH = 8
NPAIR = 4
OQ = 16
RING = 23
WARM = 5
WIDE = 2
GAP = 128.0
FLOOR = -3.0e38

FLOPS = 3 * 2 * ROWS * D * D + 3 * 2 * ROWS * H * DK * DK


def tile_tropicalattention_pa_kernel(
    tc, x, Wq, Wk, Wv, lam, Wq_trop, Wk_trop, Wv_trop, out_0, out_1, out_2
):
    nc = tc.nc
    weights = [Wq, Wk, Wv]
    outs = [out_0, out_1, out_2]
    with ExitStack() as ctx:
        const = ctx.enter_context(tc.tile_pool(name="const", bufs=1))
        rawp = ctx.enter_context(tc.tile_pool(name="rawp", bufs=2))
        grp = ctx.enter_context(tc.tile_pool(name="grp", bufs=2))
        xq = ctx.enter_context(tc.tile_pool(name="xq", bufs=1))
        wq = ctx.enter_context(tc.tile_pool(name="wq", bufs=1))
        pp = ctx.enter_context(tc.tile_pool(name="pp", bufs=2))
        work = ctx.enter_context(tc.tile_pool(name="work", bufs=RING))
        farp = ctx.enter_context(tc.tile_pool(name="farp", bufs=1))
        yp = ctx.enter_context(tc.tile_pool(name="yp", bufs=2))
        psum = ctx.enter_context(tc.psum_pool(name="psum", bufs=7))
        resid = ctx.enter_context(tc.psum_pool(name="resid", bufs=1))
        ctx.enter_context(tc.manual_schedule())

        ident = const.tile([P, P], F32, name="ident")
        make_identity(nc, ident[:])

        t_a = const.tile([P, DK], BF16, name="t_a")
        t_b = const.tile([P, DK], BF16, name="t_b")
        nc.sync.dma_start(out=t_a[0:64, :], in_=Wq_trop)
        nc.sync.dma_start(out=t_a[64:128, :], in_=Wk_trop)
        nc.sync.dma_start(out=t_b[0:64, :], in_=Wv_trop)
        nc.sync.dma_start(out=t_b[64:128, :], in_=Wv_trop)
        lam_sb = const.tile([P, CH], BF16, name="lam_sb")
        nc.sync.dma_start(out=lam_sb[:], in_=lam.rearrange("a b (m c) -> (a b m) c", c=CH))

        x_raw = []
        x_view = x.rearrange("b (p s) k -> p b (s k)", s=2)
        for half in range(2):
            raw = rawp.tile([P, 4 * D], BF16, name="x_raw%d" % half, tag="raw")
            nc.sync.dma_start(
                out=raw[:].rearrange("p (b f) -> p b f", b=2), in_=x_view[:, 2 * half : 2 * half + 2, :]
            )
            x_raw.append(raw[:])

        def load_w(j):
            view = weights[j].rearrange("(m c) k -> m (c k)", c=CH)
            if j == 0:
                both = pp.tile([P, 8 * D], BF16, name="w_raw", tag="pt")
                halves = [both[:, 0 : 4 * D], both[:, 4 * D : 8 * D]]
            else:
                halves = [rawp.tile([P, 4 * D], BF16, name="w_raw%d" % h, tag="raw")[:] for h in range(2)]
            for half in range(2):
                nc.sync.dma_start(out=halves[half], in_=view[:, half * 4 * D : (half + 1) * 4 * D])
            return halves

        def turn_words(raws, half, g, pair):
            rawf = raws[half].bitcast(F32)
            tp = psum.tile([P, 2, 2, P], F32, name="tp", tag="bank")
            for tt in range(2):
                for u in range(2):
                    col = (2 * pair + tt) * 512 + 256 * g + 128 * u
                    nc.tensor.transpose(tp[:, tt, u, :], rawf[:, col : col + P], ident[:])
            return tp

        def group_words(grouped, tp, pair, copy):
            gf = grouped[:].bitcast(F32)
            copy(
                out=gf[:, pair * 512 : (pair + 1) * 512].rearrange("q (t n u) -> q t n u", t=2, u=2),
                in_=tp[:].rearrange("q t u n -> q t n u"),
            )

        def new_grouped():
            return grp.tile([P, 2048], BF16, name="grouped", tag="grouped", align_bytes=64)

        def quantise(grouped, codes, scales, half, g):
            nc.vector.quantize_mx(
                out=codes[g][:, half * 512 : (half + 1) * 512].bitcast(FP8X4),
                scales=scales[g][:, half * 512 : (half + 1) * 512],
                in_=grouped[:],
            )

        def group_quarter(raws, half, g):
            grouped = new_grouped()
            for pair in range(2):
                group_words(grouped, turn_words(raws, half, g, pair), pair, nc.scalar.copy)
            return grouped

        w_raw0 = load_w(0)

        lam_f = const.tile([P, CH], F32, name="lam_f")
        nc.vector.tensor_copy(out=lam_f[:], in_=lam_sb[:])
        tl = const.tile([P, 3, CH, DK], F32, name="tl")
        reps = []
        for t_sb in (t_a, t_b):
            rep = work.tile([P, CH, H, CH], F32, name="rep", tag="u")
            nc.vector.tensor_copy(
                out=rep[:],
                in_=t_sb[:].rearrange("p (a c) -> p c a", c=CH).unsqueeze(2).to_broadcast([P, CH, H, CH]),
            )
            reps.append(rep)
        for which in range(2):
            for quad in range(2):
                tq = psum.tile([P, 4, P], F32, name="tq", tag="bank")
                for cc in range(4):
                    nc.tensor.transpose(
                        tq[:, cc, :], reps[which][:, 4 * quad + cc, :, :].rearrange("p h a -> p (h a)"), ident[:]
                    )
                for cc in range(4):
                    c = 4 * quad + cc
                    if which == 0:
                        out = tl[:, 0:2, c, :]
                        in0 = tq[:, cc, :].rearrange("p (j o) -> p j o", j=2)
                    else:
                        out = tl[:, 2, c, :]
                        in0 = tq[:, cc, 0:DK]
                    nc.vector.tensor_scalar(
                        out=out, in0=in0, scalar1=lam_f[:, c : c + 1], scalar2=FLOOR, op0=ALU.subtract, op1=ALU.max
                    )

        top4 = const.tile([P, 3, 4, DK], F32, name="top4")
        dt = const.tile([P, 3, NPAIR, DK], F32, name="dt")
        qd = const.tile([P, 2, 3, DK], F32, name="qd")

        def highest(out, in0, in1):
            nc.vector.tensor_tensor(out=out, in0=in0, in1=in1, op=ALU.max)

        def less(out, in0, in1):
            nc.vector.tensor_tensor(out=out, in0=in0, in1=in1, op=ALU.subtract)

        def raise_low(j):
            nc.vector.scalar_tensor_tensor(
                out=tl[:, j, :, :],
                in0=top4[:, j, 0, :].unsqueeze(1).to_broadcast([P, CH, DK]),
                scalar=-GAP,
                in1=tl[:, j, :, :],
                op0=ALU.add,
                op1=ALU.max,
            )

        pairs = tl[:].rearrange("p j (q e) o -> p (j q) e o", e=2)
        table_steps = [
            lambda: highest(top4[:], tl[:, :, 0:4, :], tl[:, :, 4:8, :]),
            lambda: highest(top4[:, :, 0:2, :], top4[:, :, 0:2, :], top4[:, :, 2:4, :]),
            lambda: highest(top4[:, :, 0, :], top4[:, :, 0, :], top4[:, :, 1, :]),
            lambda: raise_low(0),
            lambda: raise_low(1),
            lambda: raise_low(2),
            lambda: less(dt[:].rearrange("p j q o -> p (j q) o"), pairs[:, :, 1, :], pairs[:, :, 0, :]),
            lambda: [less(qd[:, k, :, :], tl[:, :, 2 * k, :], tl[:, :, 2 + k, :]) for k in range(2)],
        ]

        x_codes = [xq.tile([P, ROWS], U32, name="x_codes%d" % g, align_bytes=64) for g in range(2)]
        x_scales = [xq.tile([P, ROWS], U8, name="x_scales%d" % g, align_bytes=64) for g in range(2)]
        for half in range(2):
            for g in range(2):
                quantise(group_quarter(x_raw, half, g), x_codes, x_scales, half, g)
                table_steps.pop(0)()

        def new_w():
            codes = [wq.tile([P, ROWS], U32, name="w_codes%d" % g, align_bytes=64) for g in range(2)]
            scales = [wq.tile([P, ROWS], U8, name="w_scales%d" % g, align_bytes=64) for g in range(2)]
            return codes, scales

        def new_p():
            return pp.tile([P, CH, ROWS], F32, name="pt", tag="pt")

        def multiply(w, c, rh):
            codes, scales = w
            z = psum.tile([P, 512], F32, name="z", tag="bank")
            for g in range(2):
                nc.tensor.matmul_mx(
                    out=z[:],
                    lhsT=codes[g][:, c * P : (c + 1) * P].bitcast(FP8X4),
                    lhsT_scale=scales[g][:, c * P : (c + 1) * P],
                    rhs=x_codes[g][:, rh * 512 : (rh + 1) * 512].bitcast(FP8X4),
                    rhs_scale=x_scales[g][:, rh * 512 : (rh + 1) * 512],
                    start=(g == 0),
                    stop=(g == 1),
                )
            return z

        def relu_v(pt, c, rh, z):
            nc.vector.tensor_scalar_max(out=pt[:, c, rh * 512 : (rh + 1) * 512], in0=z[:], scalar1=0.0)

        def log(pt, c, cols):
            nc.scalar.activation(out=pt[:, c, cols], in_=pt[:, c, cols], func=ACT.Ln, bias=1.0, scale=1.0)

        def odd_difference(eng, pt, c):
            eng.tensor_tensor(out=pt[:, c, :], in0=pt[:, c, :], in1=pt[:, c - 1, :], op=ALU.subtract)

        WR = WIDE * P

        def far_differences(eng, pt):
            far = farp.tile([P, 2, WR], F32, name="far", tag="far")
            eng.tensor_tensor(out=far[:, 0, :], in0=pt[:, 2, 0:WR], in1=pt[:, 0, 0:WR], op=ALU.subtract)
            eng.tensor_tensor(out=far[:, 1, :], in0=pt[:, 3, 0:WR], in1=far[:, 0, :], op=ALU.add)
            return far

        def turn_far(far, copy):
            turned = farp.tile([P, 2, WIDE, P], F32, name="turned", tag="turned")
            for k in range(2):
                bank = psum.tile([P, WIDE, P], F32, name="tr", tag="bank")
                for t in range(WIDE):
                    nc.tensor.transpose(bank[:, t, :], far[:, k, t * P : (t + 1) * P], ident[:])
                copy(out=turned[:, k, :, :], in_=bank[:])
            return turned

        def settle(turned):
            bank = resid.tile([P, 2, WR], F32, name="settled", tag="settled")
            for k in range(2):
                for t in range(WIDE):
                    nc.tensor.transpose(bank[:, k, t * P : (t + 1) * P], turned[:, k, t, :], ident[:])
            return bank

        def relu_part(out, in_, step):
            nc.scalar.activation(out=out, in_=in_, func=ACT.Relu, bias=step, scale=1.0)

        def base_part(on_scalar, out, in_, col):
            if on_scalar:
                nc.scalar.activation(out=out, in_=in_, func=ACT.Identity, bias=col, scale=1.0)
            else:
                nc.gpsimd.tensor_scalar(out=out, in0=in_, scalar1=col, scalar2=1.0, op0=ALU.add, op1=ALU.mult)

        def base_of(j, o, pt, us, q):
            lo = WR if q < 2 else 0
            base_part(q == 1 and o % 3 == 1, us[:, lo:ROWS], pt[:, 2 * q, lo:ROWS], tl[:, j, 2 * q, o : o + 1])
            if q == 0:
                base_part(True, us[:, 0:WR], pt[:, 0, 0:WR], tl[:, j, 3, o : o + 1])

        def relu_of(j, o, pt, gs, q):
            lo = WR if q == 1 else 0
            relu_part(gs[:, lo:ROWS], pt[:, 2 * q + 1, lo:ROWS], dt[:, j, q, o : o + 1])

        def prepare(j, o, pt):
            first = []
            second = []
            for q in range(NPAIR):
                us = work.tile([P, ROWS], F32, name="us", tag="u")
                gs = work.tile([P, ROWS], F32, name="gs", tag="u")
                relu_of(j, o, pt, gs, q)
                base_of(j, o, pt, us, q)
                first.append(us)
                second.append(gs)
            return first, second

        def widen(j, o, settled, gs, k):
            nc.vector.scalar_tensor_tensor(
                out=gs[:, 0:WR],
                in0=gs[:, 0:WR],
                scalar=qd[:, k, j, o : o + 1],
                in1=settled[:, k, :],
                op0=ALU.add,
                op1=ALU.max,
            )

        w = new_w()
        pt = new_p()
        quarters = [(half, g) for half in range(2) for g in range(2)]

        def quantise_w0(n):
            half, g = quarters[n]
            quantise(group_quarter(w_raw0, half, g), w[0], w[1], half, g)
            table_steps.pop(0)()

        def chunk0(c):
            zs = [multiply(w, c, rh) for rh in range(2)]
            for rh in range(2):
                relu_v(pt, c, rh, zs[rh])

        for n in range(3):
            quantise_w0(n)
        chunk0(0)
        quantise_w0(3)
        chunk0(1)
        log(pt, 0, slice(0, ROWS))
        first = []
        second = []
        for c in range(1, CH):
            if c + 1 < CH:
                chunk0(c + 1)
            log(pt, c, slice(0, ROWS))
            if c == 6:
                odd_difference(nc.vector, pt, 5)
            if c % 2 == 1:
                q = c // 2
                us = work.tile([P, ROWS], F32, name="us", tag="u")
                gs = work.tile([P, ROWS], F32, name="gs", tag="u")
                base_of(0, 0, pt, us, q)
                if q < 2:
                    odd_difference(nc.gpsimd, pt, c)
                first.append(us)
                second.append(gs)
            elif c > 2:
                relu_of(0, 0, pt, second[c // 2 - 2], c // 2 - 2)
        odd_difference(nc.vector, pt, 7)
        for q in range(2, NPAIR):
            relu_of(0, 0, pt, second[q], q)
        settled = settle(turn_far(far_differences(nc.vector, pt), nc.vector.tensor_copy))
        warm = const.tile([P, 512], BF16, name="warm")
        nc.vector.tensor_copy(out=warm[:], in_=second[2][:, 0:512])
        bank = psum.tile([P, 512], F32, name="warm_bank", tag="bank")
        for k in range(WARM):
            nc.tensor.matmul(out=bank[:], lhsT=warm[:, 0:P], rhs=warm[:], start=True, stop=True)
        ready = [(first, second), prepare(0, 1, pt)]
        for o in range(2):
            for k in range(2):
                widen(0, o, settled, ready[o][1][0], k)

        w_raws = {1: load_w(1)}

        for j in range(3):
            out_view = outs[j].rearrange("n (p s) o -> p n s o", s=2)
            if j < 2:
                w_raw = w_raws[j + 1]
                w_next = new_w()
                next_p = new_p()
            grouped = None
            z = None
            logs = []
            for o in range(DK):
                oq, ol = divmod(o, OQ)
                if ol == 0:
                    y = yp.tile([P, 2, 4, H, OQ], F32, name="y", tag="y")
                first, second = ready.pop(0)
                nj, no = (j, o + 2) if o + 2 < DK else (j + 1, o + 2 - DK)
                if nj < 3:
                    ready.append(prepare(nj, no, pt if nj == j else next_p))
                for c, rh in logs:
                    log(next_p, c, slice(rh * 512, (rh + 1) * 512))
                    if c % 2 == 1 and rh == 1:
                        odd_difference(nc.gpsimd, next_p, c)
                    if c == 3 and rh == 1:
                        far = far_differences(nc.gpsimd, next_p)
                logs = []
                blocks = []
                for t in range(8):
                    if no == 0 and nj < 3 and t == 3:
                        settled = settle(turned)
                    used = [0, 2, 3] if t < WIDE else [0, 1, 2, 3]
                    ft = psum.tile([P, len(used), P], F32, name="ft", tag="bank")
                    blocks.append((t, ft))
                    cols = slice(t * P, (t + 1) * P)
                    for n, q in enumerate(used):
                        nc.tensor.matmul(
                            out=ft[:, n, :], lhsT=first[q][:, cols], rhs=ident[:],
                            start=True, stop=False, is_transpose=True,
                        )
                        nc.tensor.matmul(
                            out=ft[:, n, :], lhsT=second[q][:, cols], rhs=ident[:],
                            start=False, stop=True, is_transpose=True,
                        )
                    if t % 2 == 1:
                        for tb, fb in reversed(blocks):
                            nc.vector.tensor_reduce(
                                out=y[:, tb % 2, tb // 2, :, ol],
                                in_=fb[:].rearrange("p q (h a) -> p h q a", a=CH),
                                axis=mybir.AxisListType.XY,
                                op=ALU.max,
                            )
                        blocks = []
                    if nj < 3 and t in (5, 7):
                        widen(nj, no, settled, ready[1][1][0], (t - 5) // 2)
                    if j == 2 and o == DK - 1 and t % 2 == 1:
                        b = t // 2
                        for s in range(2):
                            nc.sync.dma_start(
                                out=out_view[:, H * b : H * (b + 1), s, oq * OQ : (oq + 1) * OQ], in_=y[:, s, b, :, :]
                            )
                    if j < 2:
                        if 1 <= o < 17:
                            eighth, late = divmod(o - 1, 2)
                            quarter, pair = divmod(eighth, 2)
                            half, g = divmod(quarter, 2)
                            if late == 0 and t == 4:
                                tp = turn_words(w_raw, half, g, pair)
                            if late == 0 and t == 5:
                                if pair == 0:
                                    grouped = new_grouped()
                                group_words(grouped, tp, pair, nc.vector.tensor_copy)
                            if late == 1 and pair == 1 and t == 3:
                                quantise(grouped, w_next[0], w_next[1], half, g)
                        elif 17 <= o < 33:
                            c, rh = divmod(o - 17, 2)
                            if t == 4:
                                z = multiply(w_next, c, rh)
                            if t == 5:
                                relu_v(next_p, c, rh, z)
                                logs.append((c, rh))
                        elif o == 34 and t == 0 and j == 0:
                            w_raws[2] = load_w(2)
                        elif o == 38 and t == 3:
                            turned = turn_far(far, nc.vector.tensor_copy)
                if ol == OQ - 1 and not (j == 2 and o == DK - 1):
                    y_view = y[:].rearrange("p s b h o -> p s (b h) o")
                    for s in range(2):
                        nc.sync.dma_start(out=out_view[:, :, s, oq * OQ : (oq + 1) * OQ], in_=y_view[:, s, :, :])
            if j < 2:
                pt = next_p
